import numpy as np
import ml_dtypes


def mxq(x, axis, fmt="e4m3"):
    dtype, down = {"e4m3": (ml_dtypes.float8_e4m3fn, 7), "e5m2": (ml_dtypes.float8_e5m2, 14)}[fmt]
    v = np.moveaxis(np.asarray(x, np.float32).astype(ml_dtypes.bfloat16).astype(np.float64), axis, -1)
    blocks = v.reshape(v.shape[:-1] + (-1, 32))
    amax = np.abs(blocks).max(-1, keepdims=True)
    byte = np.maximum(np.where(amax > 0, np.frexp(amax)[1] - 1 + 127, 0) - down, 1)
    scale = np.exp2(byte - 127.0)
    codes = (blocks / scale).astype(np.float32).astype(dtype).astype(np.float64)
    return np.moveaxis((codes * scale).reshape(v.shape), -1, axis)


WIDE = False


def mx_kscale(k):
    if not WIDE:
        return np.ones(k)
    levels = np.array([10, -10, 5, -5, 0])
    if k % 512:
        return np.exp2(np.random.permutation(np.resize(levels, k // 32))).repeat(32)
    a = np.empty((k // 512, 16))
    for p in range(k // 512):
        a[p, :8] = np.random.permutation(np.resize(levels, 8))
        for g in range(8):
            far = levels[np.abs(levels - a[p, g]) >= 10]
            a[p, g + 8] = far[np.random.randint(len(far))]
    return np.exp2(a.ravel()).repeat(32)


BF16 = ml_dtypes.bfloat16


def bf(x):
    return np.asarray(x, np.float32).astype(BF16)


def f64(x):
    return np.asarray(x).astype(np.float64)


B, P, D, NL, T, E, G = 2, 192, 1024, 16, 2, 1, 2
WG = NL * NL * T * G
CLIP = 1.0
LOG_2PI = np.log(2.0 * np.pi)


def clip(v):
    return np.clip(v, -CLIP, CLIP)


def gaussian_multi(m1, v1, m2, v2):
    v1s = np.exp(2.0 * v1)
    v2s = np.exp(2.0 * v2)
    add = v1s + v2s
    log_add = np.log(add)
    scale = (-0.5 * (LOG_2PI + log_add + (m1 - m2) ** 2 / add)).sum(-1)
    mu = (m1 * v2s + m2 * v1s) / add
    var = v1 + v2 - 0.5 * log_add
    return scale, mu, var


def draw0():
    s = mx_kscale(D)
    return {"x": bf(np.random.standard_normal((B, P, D)) * s),
            "s_weight": bf(np.random.standard_normal((B, P, NL, E))),
            "s_mu": bf(clip(np.random.standard_normal((B, P, NL, E, G)))),
            "s_var": bf(clip(np.random.standard_normal((B, P, NL, E, G)))),
            "tcm_w": bf(np.random.standard_normal((D, WG)) / np.sqrt(D) / s[:, None]),
            "tcm_b": bf(np.random.standard_normal(WG) * 0.3),
            "tcv_w": bf(np.random.standard_normal((D, WG)) / np.sqrt(D) / s[:, None]),
            "tcv_b": bf(np.random.standard_normal(WG) * 0.3)}


def core(x, s_weight, s_mu, s_var, tcm_w, tcm_b, tcv_w, tcv_b):
    xq = mxq(f64(x).reshape(B * P, D), 1, "e4m3")
    t_c_mu = clip(((xq @ mxq(f64(tcm_w), 0, "e4m3")) + f64(tcm_b)).reshape(B, P, NL, NL, T, G))[:, :, :, :, :, None, :]
    t_c_var = clip(((xq @ mxq(f64(tcv_w), 0, "e4m3")) + f64(tcv_b)).reshape(B, P, NL, NL, T, G))[:, :, :, :, :, None, :]
    m1 = f64(s_mu)[:, :, None, :, None, :, :]
    v1 = f64(s_var)[:, :, None, :, None, :, :]
    cs_scale, cs_mu, cs_var = gaussian_multi(m1, v1, t_c_mu, t_c_var)
    cs_scale = cs_scale + f64(s_weight)[:, :, None, :, None, :]
    return cs_scale, cs_mu, cs_var


def e4m3fn_bytes(y):
    return np.clip(np.asarray(y, np.float64), -448.0, 448.0).astype(np.float32).astype(ml_dtypes.float8_e4m3fn).view(np.uint8)


def e4m3fn_values(b):
    return np.asarray(b, np.uint8).view(ml_dtypes.float8_e4m3fn).astype(np.float64)


def setup_inputs():
    d = draw0()
    x0 = np.asarray(d['tcv_w']).astype(np.float64)
    s = (np.max(np.abs(x0), axis=(1,), keepdims=True) / 448.0).astype(np.float32)
    out = {}
    for k, v in d.items():
        if k == 'tcv_w':
            out['tcv_w_bytes'] = e4m3fn_bytes(x0 / s.astype(np.float64))
            out['tcv_w_scale'] = s
        else:
            out[k] = v
    return out


def reference(x, s_weight, s_mu, s_var, tcm_w, tcm_b, tcv_w_bytes, tcv_w_scale, tcv_b):
    return core(x, s_weight, s_mu, s_var, tcm_w, tcm_b, e4m3fn_values(tcv_w_bytes) * tcv_w_scale.astype(np.float64), tcv_b)

@@ -1,0 +1,364 @@
+from contextlib import ExitStack
+import math
+
+import concourse.mybir as mybir
+from concourse.masks import make_identity
+
+F32 = mybir.dt.float32
+BF16 = mybir.dt.bfloat16
+U8 = mybir.dt.uint8
+U32 = mybir.dt.uint32
+FP8 = mybir.dt.float8_e4m3fn
+FP8X4 = mybir.dt.float8_e4m3fn_x4
+AF = mybir.ActivationFunctionType
+ALU = mybir.AluOpType
+
+P = 128
+TOK = 384
+NA = 3
+KD = 1024
+NG = 2
+NCH = 1024
+NCT = 8
+NB = 4
+NH = 2
+HW = 512
+LOG_2PI = math.log(2.0 * math.pi)
+
+FLOPS = 2 * TOK * KD * 2 * NCH
+
+TOKEN_WINDOWS = ((0, 256), (256, 128))
+
+
+def tile_chainlveg_pa_kernel(tc, x, s_weight, s_mu, s_var, tcm_w, tcm_b,
+                                         tcv_w_bytes, tcv_w_scale, tcv_b, out_0, out_1, out_2):
+    nc = tc.nc
+
+    xv = x.rearrange("b p d -> (b p) d").rearrange("(a q) d -> q a d", q=P)
+    smv = s_mu.rearrange("b p j e g -> (b p) (j e g)").rearrange("(a q) c -> q a c", q=P)
+    svv = s_var.rearrange("b p j e g -> (b p) (j e g)").rearrange("(a q) c -> q a c", q=P)
+    swv = s_weight.rearrange("b p j e -> (b p) (j e)").rearrange("(a q) c -> q a c", q=P)
+    o0 = out_0.rearrange("b p i j t e -> (b p) (i j t e)").rearrange("(a q) c -> q a c", q=P)
+    o1 = out_1.rearrange("b p i j t e g -> (b p) (i j t e g)").rearrange("(a q) c -> q a c", q=P)
+    o2 = out_2.rearrange("b p i j t e g -> (b p) (i j t e g)").rearrange("(a q) c -> q a c", q=P)
+
+    with ExitStack() as ctx:
+        keep = ctx.enter_context(tc.tile_pool(name="keep", bufs=1))
+        front = ctx.enter_context(tc.tile_pool(name="front", bufs=NB))
+        stage = ctx.enter_context(tc.tile_pool(name="stage", bufs=3))
+        pmx = ctx.enter_context(tc.psum_pool(name="pmx", bufs=1))
+        ptr = ctx.enter_context(tc.psum_pool(name="ptr", bufs=2))
+        psm = ctx.enter_context(tc.psum_pool(name="psm", bufs=4))
+
+        sv = keep.tile([P, NA, 32], BF16, name="sv")
+        sm = keep.tile([P, NA, 32], BF16, name="sm")
+        sw = keep.tile([P, NA, 16], BF16, name="sw")
+        vsc = keep.tile([P, NG, 4], F32, name="vsc")
+        brow = keep.tile([P, P], BF16, name="brow")
+        nc.vector.memset(brow[:], 0.0)
+        warm = keep.tile([P, 1], F32, name="warm")
+        nc.vector.memset(warm[:], 0.0)
+        warm2 = keep.tile([P, 1], F32, name="warm2")
+        nc.scalar.activation(out=warm2[:], in_=warm[:], func=AF.Sigmoid)
+        nc.sync.dma_start(out=vsc[:], in_=tcv_w_scale.rearrange("(g p t) o -> p g (t o)", p=P, t=4))
+
+        vbytes = {}
+        rawm = {}
+        xs = keep.tile([P, NA, KD], BF16, name="xs")
+
+        def load_v(h):
+            for g in range(NG):
+                t = keep.tile([P, 4, HW], U8, name="vbytes%d%d" % (g, h))
+                nc.sync.dma_start(
+                    out=t[:],
+                    in_=tcv_w_bytes[512 * g:512 * (g + 1), HW * h:HW * (h + 1)].rearrange("(p j) n -> p j n", j=4))
+                vbytes[(g, h)] = t
+
+        def load_m(h):
+            for g in range(NG):
+                t = keep.tile([P, 4, HW], BF16, name="rawm%d%d" % (g, h))
+                nc.sync.dma_start(
+                    out=t[:],
+                    in_=tcm_w[512 * g:512 * (g + 1), HW * h:HW * (h + 1)].rearrange("(p j) n -> p j n", j=4))
+                rawm[(g, h)] = t
+
+        load_v(0)
+        nc.sync.dma_start(out=sv[:], in_=svv)
+        nc.sync.dma_start(out=sm[:], in_=smv)
+        nc.sync.dma_start(out=sw[:], in_=swv)
+        nc.sync.dma_start(out=brow[0:8, :], in_=tcm_b.rearrange("(c q) -> c q", q=P))
+        nc.sync.dma_start(out=brow[8:16, :], in_=tcv_b.rearrange("(c q) -> c q", q=P))
+        load_m(0)
+        for a in range(NA):
+            nc.sync.dma_start(out=xs[:, a, :], in_=xv[:, a, :])
+        load_v(1)
+        load_m(1)
+
+        ident = keep.tile([P, P], F32, name="ident")
+        make_identity(nc, ident[:])
+        identb = keep.tile([P, P], BF16, name="identb")
+        make_identity(nc, identb[:])
+        late_one = keep.tile([P, 1], F32, name="late_one")
+        pair = keep.tile([P, 64], F32, name="pair")
+        nc.vector.tensor_tensor(out=pair[:], in0=ident[:, 0:P:2], in1=ident[:, 1:P:2], op=ALU.add)
+        shalf = keep.tile([P, 64], F32, name="shalf")
+        nc.vector.tensor_scalar(out=shalf[:], in0=pair[:], scalar1=0.5, scalar2=None, op0=ALU.mult)
+        sneg = keep.tile([P, 64], F32, name="sneg")
+        nc.vector.tensor_scalar(out=sneg[:], in0=pair[:], scalar1=-1.0, scalar2=None, op0=ALU.mult)
+
+        sv_flat = sv[:].rearrange("p a c -> p (a c)")
+        sg = keep.tile([P, 96], F32, name="sg")
+        sgc = keep.tile([P, 96], F32, name="sgc")
+        nc.scalar.activation(out=sg[:], in_=sv_flat, func=AF.Sigmoid, scale=-2.0)
+        nc.scalar.activation(out=sgc[:], in_=sv_flat, func=AF.Sigmoid, scale=2.0)
+        rc = keep.tile([P, 96], F32, name="rc")
+        nc.vector.reciprocal(out=rc[:], in_=sgc[:])
+        nie = keep.tile([P, 96], F32, name="nie")
+        nc.vector.scalar_tensor_tensor(out=nie[:], in0=sg[:], scalar=-1.0, in1=rc[:], op0=ALU.mult, op1=ALU.mult)
+
+        def spread_t(dst, src2):
+            nc.vector.tensor_copy(
+                out=dst[:].rearrange("p a (j t g) -> p (a j) t g", t=2, g=2),
+                in_=src2.unsqueeze(2).to_broadcast([P, 48, 2, 2]))
+
+        m1x = keep.tile([P, NA, 64], F32, name="m1x")
+        v1x = keep.tile([P, NA, 64], F32, name="v1x")
+        nex = keep.tile([P, NA, 64], F32, name="nex")
+        spread_t(v1x, sv[:].rearrange("p a (j g) -> p (a j) g", g=2))
+        spread_t(m1x, sm[:].rearrange("p a (j g) -> p (a j) g", g=2))
+        spread_t(nex, nie[:].rearrange("p (c g) -> p c g", g=2))
+
+        bigv = keep.tile([P, NA, 2, 64], F32, name="bigv")
+        bigm = keep.tile([P, NA, 2, 64], F32, name="bigm")
+        bige = keep.tile([P, NA, 2, 64], F32, name="bige")
+        nc.vector.tensor_scalar(out=bigv[:], in0=v1x[:].unsqueeze(2).to_broadcast([P, NA, 2, 64]),
+                                scalar1=1.0, scalar2=None, op0=ALU.add)
+        nc.vector.tensor_scalar(out=bigm[:], in0=m1x[:].unsqueeze(2).to_broadcast([P, NA, 2, 64]),
+                                scalar1=1.0, scalar2=None, op0=ALU.add)
+        nc.vector.tensor_copy(out=bige[:], in_=nex[:].unsqueeze(2).to_broadcast([P, NA, 2, 64]))
+        bigd = keep.tile([P, NA, 2, 64], F32, name="bigd")
+        nc.vector.tensor_scalar(out=bigd[:], in0=v1x[:].unsqueeze(2).to_broadcast([P, NA, 2, 64]),
+                                scalar1=2.0, scalar2=2.0, op0=ALU.mult, op1=ALU.add)
+
+        tabs_ps = []
+        for big in (bigv, bigm, bige, bigd):
+            tq = psm.tile([P, TOK], F32, name="tq", tag="sums")
+            for a in range(NA):
+                nc.tensor.transpose(tq[:, a * P:(a + 1) * P], big[:, a, :, :].rearrange("p i c -> p (i c)"), ident[:])
+            tabs_ps.append(tq)
+
+        bt = ptr.tile([P, P], BF16, name="bt", tag="tr")
+        nc.tensor.transpose(bt[:], brow[:], identb[:])
+        bias1 = keep.tile([P, 16], F32, name="bias1")
+        nc.vector.tensor_scalar(out=bias1[:], in0=bt[:, 0:16], scalar1=1.0, scalar2=None, op0=ALU.add)
+
+        svp = sv[:].rearrange("p a (j g) -> p (a j) g", g=2)
+        vsum = keep.tile([P, 48], F32, name="vsum")
+        nc.vector.tensor_tensor(out=vsum[:], in0=svp[:, :, 0], in1=svp[:, :, 1], op=ALU.add)
+        t0x = keep.tile([P, NA, 32], F32, name="t0x")
+        nc.vector.scalar_tensor_tensor(
+            out=t0x[:].rearrange("p a (j t) -> p (a j) t", t=2),
+            in0=sw[:].rearrange("p a j -> p (a j)").unsqueeze(2).to_broadcast([P, 48, 2]),
+            scalar=-LOG_2PI,
+            in1=vsum[:].unsqueeze(2).to_broadcast([P, 48, 2]),
+            op0=ALU.add, op1=ALU.subtract)
+
+        wcod = {}
+        wscl = {}
+        for nm in ("m", "v"):
+            wcod[nm] = keep.tile([P, NG, NCH], U32, name="wcod" + nm, align_bytes=64)
+            wscl[nm] = keep.tile([P, NG, NCH], U8, name="wscl" + nm, align_bytes=64)
+        wide = {}
+        grouped = {}
+
+        def widen(h):
+            for g in range(NG):
+                t = keep.tile([P, 4, HW], BF16, name="wide%d%d" % (g, h))
+                for j in range(4):
+                    nc.scalar.activation(out=t[:, j, :], in_=vbytes[(g, h)][:, j, :].bitcast(FP8),
+                                         func=AF.Copy, scale=vsc[:, g, j:j + 1])
+                wide[(g, h)] = t
+
+        def interleave(nm, g, h, on_scalar):
+            src = rawm[(g, h)] if nm == "m" else wide[(g, h)]
+            t = keep.tile([P, HW, 4], BF16, name="grp%s%d%d" % (nm, g, h), align_bytes=64)
+            if on_scalar:
+                nc.scalar.copy(out=t[:], in_=src[:].rearrange("p j n -> p n j"))
+            else:
+                nc.vector.tensor_copy(out=t[:], in_=src[:].rearrange("p j n -> p n j"))
+            grouped[(nm, g, h)] = t
+
+        def quantize_w(nm, g, h):
+            cols = slice(HW * h, HW * (h + 1))
+            nc.vector.quantize_mx(out=wcod[nm][:, g, cols].bitcast(FP8X4), scales=wscl[nm][:, g, cols],
+                                  in_=grouped[(nm, g, h)][:].rearrange("p n j -> p (n j)"))
+
+        widen(0)
+
+        xg = keep.tile([P, NG, 4 * TOK], BF16, name="xg", align_bytes=64)
+        xgw = xg[:].rearrange("p g c -> p (g c)").bitcast(F32).rearrange("p (g r u) -> p g r u", g=NG, u=2)
+        xcod = keep.tile([P, NG, TOK], U32, name="xcod", align_bytes=64)
+        xscl = keep.tile([P, NG, TOK], U8, name="xscl", align_bytes=64)
+        for a in range(NA):
+            words = xs[:, a, :].bitcast(F32)
+            xt = ptr.tile([P, NG, 2, P], F32, name="xt", tag="tr")
+            for g in range(NG):
+                for u in range(2):
+                    nc.tensor.transpose(xt[:, g, u, :], words[:, 256 * g + u:256 * (g + 1):2], ident[:])
+            nc.scalar.copy(out=xgw[:, :, a * P:(a + 1) * P, :], in_=xt[:].rearrange("p g u r -> p g r u"))
+
+        tabs = []
+        for i, nm in enumerate(("v1p", "m1p", "nie1", "v1d")):
+            t = keep.tile([P, TOK], F32, name=nm)
+            nc.scalar.copy(out=t[:], in_=tabs_ps[i][:])
+            tabs.append(t)
+        v1p, m1p, nie1, v1d = tabs
+
+        for g in range(NG):
+            interleave("m", g, 0, False)
+        for g in range(NG):
+            quantize_w("m", g, 0)
+        for g in range(NG):
+            interleave("v", g, 0, False)
+        for g in range(NG):
+            for t0, tw in TOKEN_WINDOWS:
+                nc.vector.quantize_mx(out=xcod[:, g, t0:t0 + tw].bitcast(FP8X4), scales=xscl[:, g, t0:t0 + tw],
+                                      in_=xg[:, g, 4 * t0:4 * (t0 + tw)])
+        for g in range(NG):
+            quantize_w("v", g, 0)
+
+        widen(1)
+
+        dt_ = {}
+        zt_ = {}
+        st_ = {}
+        wt_ = {}
+
+        def project(ct):
+            b, c2 = divmod(ct, 2)
+            if c2 == 0:
+                dt_[b] = front.tile([P, 2, TOK], F32, name="dd", tag="dd")
+                zt_[b] = front.tile([P, 2, TOK], F32, name="zz", tag="zz")
+            cols = slice(ct * P, (ct + 1) * P)
+            for nm, tg, dst, bcol in (("v", "pv", zt_[b], 8 + ct), ("m", "pm", dt_[b], ct)):
+                acc = pmx.tile([P, TOK], F32, name="acc" + nm, tag=tg)
+                for t0, tw in TOKEN_WINDOWS:
+                    for g in range(NG):
+                        nc.tensor.matmul_mx(out=acc[:, t0:t0 + tw],
+                                            lhsT=wcod[nm][:, g, cols].bitcast(FP8X4), lhsT_scale=wscl[nm][:, g, cols],
+                                            rhs=xcod[:, g, t0:t0 + tw].bitcast(FP8X4), rhs_scale=xscl[:, g, t0:t0 + tw],
+                                            start=(g == 0), stop=(g == NG - 1))
+                nc.scalar.activation(out=dst[:, c2, :], in_=acc[:], func=AF.Relu, bias=bias1[:, bcol:bcol + 1], scale=1.0)
+
+        def both(t):
+            return t[:].unsqueeze(1).to_broadcast([P, 2, TOK])
+
+        def differences(b):
+            nc.vector.scalar_tensor_tensor(out=zt_[b][:], in0=zt_[b][:], scalar=2.0, in1=both(v1p),
+                                           op0=ALU.min, op1=ALU.subtract)
+            nc.vector.scalar_tensor_tensor(out=dt_[b][:], in0=dt_[b][:], scalar=2.0, in1=both(m1p),
+                                           op0=ALU.min, op1=ALU.subtract)
+
+        def sigmoid(b):
+            st_[b] = front.tile([P, 2, TOK], F32, name="ss", tag="ss")
+            nc.scalar.activation(out=st_[b][:], in_=zt_[b][:], func=AF.Sigmoid, scale=-2.0)
+
+        def product_w(b):
+            wt_[b] = front.tile([P, 2, TOK], F32, name="ww", tag="ww")
+            nc.vector.tensor_tensor(out=wt_[b][:], in0=dt_[b][:], in1=st_[b][:], op=ALU.mult)
+
+        def product_q(b):
+            nc.vector.tensor_tensor(out=dt_[b][:], in0=wt_[b][:], in1=dt_[b][:], op=ALU.mult)
+            nc.vector.tensor_tensor(out=dt_[b][:], in0=dt_[b][:], in1=both(nie1), op=ALU.mult)
+
+        def turn_back(src, table, spare):
+            if spare:
+                lo = pmx.tile([P, 2, 256], F32, name="lo2", tag="pm")
+                hi = pmx.tile([P, 256], F32, name="hi2", tag="pv")
+            else:
+                lo = ptr.tile([P, 2, 256], F32, name="lo", tag="tr")
+                hi = ptr.tile([P, 256], F32, name="hi", tag="tr")
+            for bank, tiles in ((lo, (0, 1)), (hi, (2,))):
+                spots = [(a, c2) for a in tiles for c2 in range(2)]
+                for k, (a, c2) in enumerate(spots):
+                    dst = bank[:, a, c2 * P:(c2 + 1) * P] if a < 2 else bank[:, c2 * P:(c2 + 1) * P]
+                    nc.tensor.matmul(out=dst, lhsT=table[:, a * P:(a + 1) * P], rhs=ident[:], is_transpose=True,
+                                     start=(k == 0), stop=False)
+                for k, (a, c2) in enumerate(spots):
+                    dst = bank[:, a, c2 * P:(c2 + 1) * P] if a < 2 else bank[:, c2 * P:(c2 + 1) * P]
+                    nc.tensor.matmul(out=dst, lhsT=src[:, c2, a * P:(a + 1) * P], rhs=ident[:], is_transpose=True,
+                                     start=False, stop=(k == len(spots) - 1))
+            return lo, hi
+
+        banks = {}
+
+        def turn_mu(b):
+            banks[("mu", b)] = turn_back(wt_[b], m1p, False)
+
+        def store_mu(b):
+            lo, hi = banks[("mu", b)]
+            res = stage.tile([P, NA, 256], F32, name="mu", tag="mu")
+            nc.scalar.activation(out=res[:, 0:2, :], in_=lo[:], func=AF.Copy, bias=-1.0, scale=1.0)
+            nc.scalar.activation(out=res[:, 2, :], in_=hi[:], func=AF.Copy, bias=-1.0, scale=1.0)
+            nc.sync.dma_start(out=o1[:, :, 256 * b:256 * (b + 1)], in_=res[:])
+
+        def logs(b):
+            nc.scalar.activation(out=st_[b][:], in_=st_[b][:], func=AF.Ln, scale=-1.0, bias=late_one[:, 0:1])
+
+        SPOTS = [(a, c2) for a in range(NA) for c2 in range(2)]
+
+        def pair_sums(b, src, mat, first, last):
+            if first:
+                banks[("sc", b)] = psm.tile([P, NA, P], F32, name="sums", tag="sums")
+            sums = banks[("sc", b)]
+            for k, (a, c2) in enumerate(SPOTS):
+                nc.tensor.matmul(out=sums[:, a, c2 * 64:(c2 + 1) * 64], lhsT=src[:, c2, a * P:(a + 1) * P], rhs=mat[:],
+                                 start=(first and k == 0), stop=(last and k == len(SPOTS) - 1))
+
+        def turn_var_scale(b):
+            banks[("var", b)] = turn_back(st_[b], v1d, b % 2 == 1)
+            pair_sums(b, st_[b], shalf, False, True)
+
+        def store_var_scale(b):
+            lo, hi = banks[("var", b)]
+            res = stage.tile([P, NA, 256], F32, name="var", tag="var")
+            nc.scalar.activation(out=res[:, 0:2, :], in_=lo[:], func=AF.Copy, bias=-1.0, scale=0.5)
+            nc.scalar.activation(out=res[:, 2, :], in_=hi[:], func=AF.Copy, bias=-1.0, scale=0.5)
+            nc.sync.dma_start(out=o2[:, :, 256 * b:256 * (b + 1)], in_=res[:])
+            sums = banks[("sc", b)]
+            res0 = stage.tile([P, NA, P], F32, name="sc", tag="sc")
+            nc.vector.tensor_tensor(out=res0[:].rearrange("p a (i c) -> p a i c", i=4),
+                                    in0=sums[:].rearrange("p a (i c) -> p a i c", i=4),
+                                    in1=t0x[:].unsqueeze(2).to_broadcast([P, NA, 4, 32]), op=ALU.add)
+            nc.sync.dma_start(out=o0[:, :, P * b:P * (b + 1)], in_=res0[:])
+
+        def to_mu(b):
+            differences(b)
+            sigmoid(b)
+            pair_sums(b, zt_[b], sneg, True, False)
+            product_w(b)
+            turn_mu(b)
+            store_mu(b)
+
+        for ct in range(4):
+            project(ct)
+        to_mu(0)
+        to_mu(1)
+        for nm in ("m", "v"):
+            for g in range(NG):
+                interleave(nm, g, 1, False)
+            for g in range(NG):
+                quantize_w(nm, g, 1)
+        for ct in range(4, 8):
+            project(ct)
+        to_mu(2)
+        to_mu(3)
+        nc.vector.tensor_scalar(out=late_one[:], in0=st_[NB - 1][:, 0, 0:1], scalar1=0.0, scalar2=1.0,
+                                op0=ALU.mult, op1=ALU.add)
+        for b in range(NB):
+            product_q(b)
+            pair_sums(b, dt_[b], shalf, False, False)
+        for b in range(NB):
+            logs(b)
+            turn_var_scale(b)
+            store_var_scale(b)

@@ -19,15 +19,14 @@ NA = 3
 KD = 1024
 NG = 2
 NCH = 1024
-NCT = 8
 NB = 4
-NH = 2
-HW = 512
 LOG_2PI = math.log(2.0 * math.pi)
 
 FLOPS = 2 * TOK * KD * 2 * NCH
 
 TOKEN_WINDOWS = ((0, 256), (256, 128))
+CHUNKS = ((0, 512), (512, 512))
+SPOTS = [(a, c2) for a in range(NA) for c2 in range(2)]
 
 
 def tile_chainlveg_pa_kernel(tc, x, s_weight, s_mu, s_var, tcm_w, tcm_b,
@@ -60,39 +59,37 @@ def tile_chainlveg_pa_kernel(tc, x, s_weight, s_mu, s_var, tcm_w, tcm_b,
         nc.vector.memset(warm[:], 0.0)
         warm2 = keep.tile([P, 1], F32, name="warm2")
         nc.scalar.activation(out=warm2[:], in_=warm[:], func=AF.Sigmoid)
-        nc.sync.dma_start(out=vsc[:], in_=tcv_w_scale.rearrange("(g p t) o -> p g (t o)", p=P, t=4))
 
         vbytes = {}
         rawm = {}
         xs = keep.tile([P, NA, KD], BF16, name="xs")
 
-        def load_v(h):
-            for g in range(NG):
-                t = keep.tile([P, 4, HW], U8, name="vbytes%d%d" % (g, h))
-                nc.sync.dma_start(
-                    out=t[:],
-                    in_=tcv_w_bytes[512 * g:512 * (g + 1), HW * h:HW * (h + 1)].rearrange("(p j) n -> p j n", j=4))
-                vbytes[(g, h)] = t
+        def load_w(nm, q, gs=(0, 1)):
+            c0, cw = CHUNKS[q]
+            for g in gs:
+                if nm == "v":
+                    t = keep.tile([P, 4, cw], U8, name="vbytes%d%d" % (g, q))
+                    src = tcv_w_bytes
+                    vbytes[(g, q)] = t
+                else:
+                    t = keep.tile([P, 4, cw], BF16, name="rawm%d%d" % (g, q))
+                    src = tcm_w
+                    rawm[(g, q)] = t
+                nc.sync.dma_start(out=t[:], in_=src[512 * g:512 * (g + 1), c0:c0 + cw].rearrange("(p j) n -> p j n", j=4))
 
-        def load_m(h):
-            for g in range(NG):
-                t = keep.tile([P, 4, HW], BF16, name="rawm%d%d" % (g, h))
-                nc.sync.dma_start(
-                    out=t[:],
-                    in_=tcm_w[512 * g:512 * (g + 1), HW * h:HW * (h + 1)].rearrange("(p j) n -> p j n", j=4))
-                rawm[(g, h)] = t
-
-        load_v(0)
+        nc.sync.dma_start(out=vsc[:], in_=tcv_w_scale.rearrange("(g p t) o -> p g (t o)", p=P, t=4))
+        load_w("m", 0, (0,))
+        load_w("v", 0)
+        load_w("m", 0, (1,))
+        for a in range(NA):
+            nc.sync.dma_start(out=xs[:, a, :], in_=xv[:, a, :])
+        nc.sync.dma_start(out=brow[0:8, :], in_=tcm_b.rearrange("(c q) -> c q", q=P))
+        nc.sync.dma_start(out=brow[8:16, :], in_=tcv_b.rearrange("(c q) -> c q", q=P))
         nc.sync.dma_start(out=sv[:], in_=svv)
         nc.sync.dma_start(out=sm[:], in_=smv)
         nc.sync.dma_start(out=sw[:], in_=swv)
-        nc.sync.dma_start(out=brow[0:8, :], in_=tcm_b.rearrange("(c q) -> c q", q=P))
-        nc.sync.dma_start(out=brow[8:16, :], in_=tcv_b.rearrange("(c q) -> c q", q=P))
-        load_m(0)
-        for a in range(NA):
-            nc.sync.dma_start(out=xs[:, a, :], in_=xv[:, a, :])
-        load_v(1)
-        load_m(1)
+        load_w("m", 1)
+        load_w("v", 1)
 
         ident = keep.tile([P, P], F32, name="ident")
         make_identity(nc, ident[:])
@@ -103,65 +100,63 @@ def tile_chainlveg_pa_kernel(tc, x, s_weight, s_mu, s_var, tcm_w, tcm_b,
         nc.vector.tensor_tensor(out=pair[:], in0=ident[:, 0:P:2], in1=ident[:, 1:P:2], op=ALU.add)
         shalf = keep.tile([P, 64], F32, name="shalf")
         nc.vector.tensor_scalar(out=shalf[:], in0=pair[:], scalar1=0.5, scalar2=None, op0=ALU.mult)
-        sneg = keep.tile([P, 64], F32, name="sneg")
-        nc.vector.tensor_scalar(out=sneg[:], in0=pair[:], scalar1=-1.0, scalar2=None, op0=ALU.mult)
 
-        sv_flat = sv[:].rearrange("p a c -> p (a c)")
+        m1x = keep.tile([P, NA, 64], F32, name="m1x")
+        v1x = keep.tile([P, NA, 64], F32, name="v1x")
+        nex = keep.tile([P, NA, 64], F32, name="nex")
+        t0x = keep.tile([P, NA, 32], F32, name="t0x")
+        bias1 = keep.tile([P, 16], F32, name="bias1")
+        v1p = keep.tile([P, TOK], F32, name="v1p")
+        m1p = keep.tile([P, TOK], F32, name="m1p")
+        nie1 = keep.tile([P, TOK], F32, name="nie1")
         sg = keep.tile([P, 96], F32, name="sg")
         sgc = keep.tile([P, 96], F32, name="sgc")
-        nc.scalar.activation(out=sg[:], in_=sv_flat, func=AF.Sigmoid, scale=-2.0)
-        nc.scalar.activation(out=sgc[:], in_=sv_flat, func=AF.Sigmoid, scale=2.0)
-        rc = keep.tile([P, 96], F32, name="rc")
-        nc.vector.reciprocal(out=rc[:], in_=sgc[:])
-        nie = keep.tile([P, 96], F32, name="nie")
-        nc.vector.scalar_tensor_tensor(out=nie[:], in0=sg[:], scalar=-1.0, in1=rc[:], op0=ALU.mult, op1=ALU.mult)
+
+        def bias_columns():
+            bt = ptr.tile([P, P], BF16, name="bt", tag="tr")
+            nc.tensor.transpose(bt[:], brow[:], identb[:])
+            nc.vector.tensor_scalar(out=bias1[:], in0=bt[:, 0:16], scalar1=1.0, scalar2=None, op0=ALU.add)
 
         def spread_t(dst, src2):
             nc.vector.tensor_copy(
                 out=dst[:].rearrange("p a (j t g) -> p (a j) t g", t=2, g=2),
                 in_=src2.unsqueeze(2).to_broadcast([P, 48, 2, 2]))
 
-        m1x = keep.tile([P, NA, 64], F32, name="m1x")
-        v1x = keep.tile([P, NA, 64], F32, name="v1x")
-        nex = keep.tile([P, NA, 64], F32, name="nex")
-        spread_t(v1x, sv[:].rearrange("p a (j g) -> p (a j) g", g=2))
-        spread_t(m1x, sm[:].rearrange("p a (j g) -> p (a j) g", g=2))
-        spread_t(nex, nie[:].rearrange("p (c g) -> p c g", g=2))
-
-        bigv = keep.tile([P, NA, 2, 64], F32, name="bigv")
-        bigm = keep.tile([P, NA, 2, 64], F32, name="bigm")
-        bige = keep.tile([P, NA, 2, 64], F32, name="bige")
-        nc.vector.tensor_scalar(out=bigv[:], in0=v1x[:].unsqueeze(2).to_broadcast([P, NA, 2, 64]),
-                                scalar1=1.0, scalar2=None, op0=ALU.add)
-        nc.vector.tensor_scalar(out=bigm[:], in0=m1x[:].unsqueeze(2).to_broadcast([P, NA, 2, 64]),
-                                scalar1=1.0, scalar2=None, op0=ALU.add)
-        nc.vector.tensor_copy(out=bige[:], in_=nex[:].unsqueeze(2).to_broadcast([P, NA, 2, 64]))
-        bigd = keep.tile([P, NA, 2, 64], F32, name="bigd")
-        nc.vector.tensor_scalar(out=bigd[:], in0=v1x[:].unsqueeze(2).to_broadcast([P, NA, 2, 64]),
-                                scalar1=2.0, scalar2=2.0, op0=ALU.mult, op1=ALU.add)
-
-        tabs_ps = []
-        for big in (bigv, bigm, bige, bigd):
+        def turned_table(label, dst, src, mul, add):
+            big = keep.tile([P, NA, 2, 64], F32, name="big" + label)
+            nc.scalar.activation(out=big[:], in_=src[:].unsqueeze(2).to_broadcast([P, NA, 2, 64]), func=AF.Copy,
+                                 scale=mul, bias=add)
             tq = psm.tile([P, TOK], F32, name="tq", tag="sums")
             for a in range(NA):
                 nc.tensor.transpose(tq[:, a * P:(a + 1) * P], big[:, a, :, :].rearrange("p i c -> p (i c)"), ident[:])
-            tabs_ps.append(tq)
+            nc.scalar.copy(out=dst[:], in_=tq[:])
 
-        bt = ptr.tile([P, P], BF16, name="bt", tag="tr")
-        nc.tensor.transpose(bt[:], brow[:], identb[:])
-        bias1 = keep.tile([P, 16], F32, name="bias1")
-        nc.vector.tensor_scalar(out=bias1[:], in0=bt[:, 0:16], scalar1=1.0, scalar2=None, op0=ALU.add)
+        def tables():
+            sv_flat = sv[:].rearrange("p a c -> p (a c)")
+            nc.scalar.activation(out=sg[:], in_=sv_flat, func=AF.Sigmoid, scale=-2.0)
+            nc.scalar.activation(out=sgc[:], in_=sv_flat, func=AF.Sigmoid, scale=2.0)
+            spread_t(v1x, sv[:].rearrange("p a (j g) -> p (a j) g", g=2))
+            turned_table("v1p", v1p, v1x, 1.0, 1.0)
+            spread_t(m1x, sm[:].rearrange("p a (j g) -> p (a j) g", g=2))
+            turned_table("m1p", m1p, m1x, 1.0, 1.0)
 
-        svp = sv[:].rearrange("p a (j g) -> p (a j) g", g=2)
-        vsum = keep.tile([P, 48], F32, name="vsum")
-        nc.vector.tensor_tensor(out=vsum[:], in0=svp[:, :, 0], in1=svp[:, :, 1], op=ALU.add)
-        t0x = keep.tile([P, NA, 32], F32, name="t0x")
-        nc.vector.scalar_tensor_tensor(
-            out=t0x[:].rearrange("p a (j t) -> p (a j) t", t=2),
-            in0=sw[:].rearrange("p a j -> p (a j)").unsqueeze(2).to_broadcast([P, 48, 2]),
-            scalar=-LOG_2PI,
-            in1=vsum[:].unsqueeze(2).to_broadcast([P, 48, 2]),
-            op0=ALU.add, op1=ALU.subtract)
+        def tables_late():
+            rc = keep.tile([P, 96], F32, name="rc")
+            nc.vector.reciprocal(out=rc[:], in_=sgc[:])
+            nie = keep.tile([P, 96], F32, name="nie")
+            nc.vector.scalar_tensor_tensor(out=nie[:], in0=sg[:], scalar=-1.0, in1=rc[:], op0=ALU.mult, op1=ALU.mult)
+            spread_t(nex, nie[:].rearrange("p (c g) -> p c g", g=2))
+            turned_table("nie1", nie1, nex, 1.0, 0.0)
+            nc.vector.tensor_copy(out=v1x4[:], in_=v1x[:].unsqueeze(2).to_broadcast([P, NA, 4, 64]))
+            svp = sv[:].rearrange("p a (j g) -> p (a j) g", g=2)
+            vsum = keep.tile([P, 48], F32, name="vsum")
+            nc.vector.tensor_tensor(out=vsum[:], in0=svp[:, :, 0], in1=svp[:, :, 1], op=ALU.add)
+            nc.vector.scalar_tensor_tensor(
+                out=t0x[:].rearrange("p a (j t) -> p (a j) t", t=2),
+                in0=sw[:].rearrange("p a j -> p (a j)").unsqueeze(2).to_broadcast([P, 48, 2]),
+                scalar=-LOG_2PI,
+                in1=vsum[:].unsqueeze(2).to_broadcast([P, 48, 2]),
+                op0=ALU.add, op1=ALU.subtract)
 
         wcod = {}
         wscl = {}
@@ -171,68 +166,54 @@ def tile_chainlveg_pa_kernel(tc, x, s_weight, s_mu, s_var, tcm_w, tcm_b,
         wide = {}
         grouped = {}
 
-        def widen(h):
+        def widen(q):
+            cw = CHUNKS[q][1]
             for g in range(NG):
-                t = keep.tile([P, 4, HW], BF16, name="wide%d%d" % (g, h))
+                t = keep.tile([P, 4, cw], BF16, name="wide%d%d" % (g, q))
                 for j in range(4):
-                    nc.scalar.activation(out=t[:, j, :], in_=vbytes[(g, h)][:, j, :].bitcast(FP8),
+                    nc.scalar.activation(out=t[:, j, :], in_=vbytes[(g, q)][:, j, :].bitcast(FP8),
                                          func=AF.Copy, scale=vsc[:, g, j:j + 1])
-                wide[(g, h)] = t
+                wide[(g, q)] = t
 
-        def interleave(nm, g, h, on_scalar):
-            src = rawm[(g, h)] if nm == "m" else wide[(g, h)]
-            t = keep.tile([P, HW, 4], BF16, name="grp%s%d%d" % (nm, g, h), align_bytes=64)
-            if on_scalar:
-                nc.scalar.copy(out=t[:], in_=src[:].rearrange("p j n -> p n j"))
-            else:
+        def interleave(nm, q):
+            cw = CHUNKS[q][1]
+            for g in range(NG):
+                src = rawm[(g, q)] if nm == "m" else wide[(g, q)]
+                t = keep.tile([P, cw, 4], BF16, name="grp%s%d%d" % (nm, g, q), align_bytes=64)
                 nc.vector.tensor_copy(out=t[:], in_=src[:].rearrange("p j n -> p n j"))
-            grouped[(nm, g, h)] = t
+                grouped[(nm, g, q)] = t
 
-        def quantize_w(nm, g, h):
-            cols = slice(HW * h, HW * (h + 1))
-            nc.vector.quantize_mx(out=wcod[nm][:, g, cols].bitcast(FP8X4), scales=wscl[nm][:, g, cols],
-                                  in_=grouped[(nm, g, h)][:].rearrange("p n j -> p (n j)"))
-
-        widen(0)
+        def quantize_w(nm, q):
+            c0, cw = CHUNKS[q]
+            for g in range(NG):
+                nc.vector.quantize_mx(out=wcod[nm][:, g, c0:c0 + cw].bitcast(FP8X4), scales=wscl[nm][:, g, c0:c0 + cw],
+                                      in_=grouped[(nm, g, q)][:].rearrange("p n j -> p (n j)"))
 
         xg = keep.tile([P, NG, 4 * TOK], BF16, name="xg", align_bytes=64)
         xgw = xg[:].rearrange("p g c -> p (g c)").bitcast(F32).rearrange("p (g r u) -> p g r u", g=NG, u=2)
         xcod = keep.tile([P, NG, TOK], U32, name="xcod", align_bytes=64)
         xscl = keep.tile([P, NG, TOK], U8, name="xscl", align_bytes=64)
-        for a in range(NA):
-            words = xs[:, a, :].bitcast(F32)
-            xt = ptr.tile([P, NG, 2, P], F32, name="xt", tag="tr")
-            for g in range(NG):
-                for u in range(2):
-                    nc.tensor.transpose(xt[:, g, u, :], words[:, 256 * g + u:256 * (g + 1):2], ident[:])
-            nc.scalar.copy(out=xgw[:, :, a * P:(a + 1) * P, :], in_=xt[:].rearrange("p g u r -> p g r u"))
 
-        tabs = []
-        for i, nm in enumerate(("v1p", "m1p", "nie1", "v1d")):
-            t = keep.tile([P, TOK], F32, name=nm)
-            nc.scalar.copy(out=t[:], in_=tabs_ps[i][:])
-            tabs.append(t)
-        v1p, m1p, nie1, v1d = tabs
+        def turn_x():
+            for a in range(NA):
+                words = xs[:, a, :].bitcast(F32)
+                xt = ptr.tile([P, NG, 2, P], F32, name="xt", tag="tr")
+                for g in range(NG):
+                    for u in range(2):
+                        nc.tensor.transpose(xt[:, g, u, :], words[:, 256 * g + u:256 * (g + 1):2], ident[:])
+                nc.scalar.copy(out=xgw[:, :, a * P:(a + 1) * P, :], in_=xt[:].rearrange("p g u r -> p g r u"))
 
-        for g in range(NG):
-            interleave("m", g, 0, False)
-        for g in range(NG):
-            quantize_w("m", g, 0)
-        for g in range(NG):
-            interleave("v", g, 0, False)
-        for g in range(NG):
+        def quantize_x():
             for t0, tw in TOKEN_WINDOWS:
-                nc.vector.quantize_mx(out=xcod[:, g, t0:t0 + tw].bitcast(FP8X4), scales=xscl[:, g, t0:t0 + tw],
-                                      in_=xg[:, g, 4 * t0:4 * (t0 + tw)])
-        for g in range(NG):
-            quantize_w("v", g, 0)
-
-        widen(1)
+                for g in range(NG):
+                    nc.vector.quantize_mx(out=xcod[:, g, t0:t0 + tw].bitcast(FP8X4), scales=xscl[:, g, t0:t0 + tw],
+                                          in_=xg[:, g, 4 * t0:4 * (t0 + tw)])
 
         dt_ = {}
         zt_ = {}
         st_ = {}
         wt_ = {}
+        banks = {}
 
         def project(ct):
             b, c2 = divmod(ct, 2)
@@ -267,9 +248,13 @@ def tile_chainlveg_pa_kernel(tc, x, s_weight, s_mu, s_var, tcm_w, tcm_b,
             wt_[b] = front.tile([P, 2, TOK], F32, name="ww", tag="ww")
             nc.vector.tensor_tensor(out=wt_[b][:], in0=dt_[b][:], in1=st_[b][:], op=ALU.mult)
 
-        def product_q(b):
+        def product_q1(b):
             nc.vector.tensor_tensor(out=dt_[b][:], in0=wt_[b][:], in1=dt_[b][:], op=ALU.mult)
+
+        def product_q2(b):
             nc.vector.tensor_tensor(out=dt_[b][:], in0=dt_[b][:], in1=both(nie1), op=ALU.mult)
+
+        v1x4 = keep.tile([P, NA, 4, 64], F32, name="v1x4")
 
         def turn_back(src, table, spare):
             if spare:
@@ -280,17 +265,16 @@ def tile_chainlveg_pa_kernel(tc, x, s_weight, s_mu, s_var, tcm_w, tcm_b,
                 hi = ptr.tile([P, 256], F32, name="hi", tag="tr")
             for bank, tiles in ((lo, (0, 1)), (hi, (2,))):
                 spots = [(a, c2) for a in tiles for c2 in range(2)]
-                for k, (a, c2) in enumerate(spots):
-                    dst = bank[:, a, c2 * P:(c2 + 1) * P] if a < 2 else bank[:, c2 * P:(c2 + 1) * P]
-                    nc.tensor.matmul(out=dst, lhsT=table[:, a * P:(a + 1) * P], rhs=ident[:], is_transpose=True,
-                                     start=(k == 0), stop=False)
+                if table is not None:
+                    for k, (a, c2) in enumerate(spots):
+                        dst = bank[:, a, c2 * P:(c2 + 1) * P] if a < 2 else bank[:, c2 * P:(c2 + 1) * P]
+                        nc.tensor.matmul(out=dst, lhsT=table[:, a * P:(a + 1) * P], rhs=ident[:], is_transpose=True,
+                                         start=(k == 0), stop=False)
                 for k, (a, c2) in enumerate(spots):
                     dst = bank[:, a, c2 * P:(c2 + 1) * P] if a < 2 else bank[:, c2 * P:(c2 + 1) * P]
                     nc.tensor.matmul(out=dst, lhsT=src[:, c2, a * P:(a + 1) * P], rhs=ident[:], is_transpose=True,
-                                     start=False, stop=(k == len(spots) - 1))
+                                     start=(table is None and k == 0), stop=(k == len(spots) - 1))
             return lo, hi
-
-        banks = {}
 
         def turn_mu(b):
             banks[("mu", b)] = turn_back(wt_[b], m1p, False)
@@ -303,9 +287,8 @@ def tile_chainlveg_pa_kernel(tc, x, s_weight, s_mu, s_var, tcm_w, tcm_b,
             nc.sync.dma_start(out=o1[:, :, 256 * b:256 * (b + 1)], in_=res[:])
 
         def logs(b):
+            nc.scalar.activation(out=zt_[b][:], in_=st_[b][:], func=AF.Ln, scale=late_one[:, 0:1])
             nc.scalar.activation(out=st_[b][:], in_=st_[b][:], func=AF.Ln, scale=-1.0, bias=late_one[:, 0:1])
-
-        SPOTS = [(a, c2) for a in range(NA) for c2 in range(2)]
 
         def pair_sums(b, src, mat, first, last):
             if first:
@@ -316,14 +299,19 @@ def tile_chainlveg_pa_kernel(tc, x, s_weight, s_mu, s_var, tcm_w, tcm_b,
                                  start=(first and k == 0), stop=(last and k == len(SPOTS) - 1))
 
         def turn_var_scale(b):
-            banks[("var", b)] = turn_back(st_[b], v1d, b % 2 == 1)
-            pair_sums(b, st_[b], shalf, False, True)
+            banks[("var", b)] = turn_back(st_[b], None, b % 2 == 1)
+            pair_sums(b, zt_[b], shalf, False, True)
 
         def store_var_scale(b):
             lo, hi = banks[("var", b)]
             res = stage.tile([P, NA, 256], F32, name="var", tag="var")
-            nc.scalar.activation(out=res[:, 0:2, :], in_=lo[:], func=AF.Copy, bias=-1.0, scale=0.5)
-            nc.scalar.activation(out=res[:, 2, :], in_=hi[:], func=AF.Copy, bias=-1.0, scale=0.5)
+            nc.vector.scalar_tensor_tensor(out=res[:, 0:2, :].rearrange("p a c -> p (a c)"),
+                                           in0=lo[:].rearrange("p a c -> p (a c)"), scalar=0.5,
+                                           in1=v1x4[:, 0:2, :, :].rearrange("p a i c -> p (a i c)"),
+                                           op0=ALU.mult, op1=ALU.add)
+            nc.vector.scalar_tensor_tensor(out=res[:, 2, :], in0=hi[:], scalar=0.5,
+                                           in1=v1x4[:, 2, :, :].rearrange("p i c -> p (i c)"),
+                                           op0=ALU.mult, op1=ALU.add)
             nc.sync.dma_start(out=o2[:, :, 256 * b:256 * (b + 1)], in_=res[:])
             sums = banks[("sc", b)]
             res0 = stage.tile([P, NA, P], F32, name="sc", tag="sc")
@@ -335,29 +323,45 @@ def tile_chainlveg_pa_kernel(tc, x, s_weight, s_mu, s_var, tcm_w, tcm_b,
         def to_mu(b):
             differences(b)
             sigmoid(b)
-            pair_sums(b, zt_[b], sneg, True, False)
             product_w(b)
             turn_mu(b)
             store_mu(b)
 
+        def prepare(q):
+            interleave("m", q)
+            interleave("v", q)
+            quantize_w("m", q)
+            quantize_w("v", q)
+
+        widen(0)
+        interleave("m", 0)
+        quantize_w("m", 0)
+        turn_x()
+        interleave("v", 0)
+        quantize_x()
+        quantize_w("v", 0)
+        bias_columns()
+        tables()
+        widen(1)
         for ct in range(4):
             project(ct)
         to_mu(0)
         to_mu(1)
-        for nm in ("m", "v"):
-            for g in range(NG):
-                interleave(nm, g, 1, False)
-            for g in range(NG):
-                quantize_w(nm, g, 1)
+        tables_late()
+        prepare(1)
         for ct in range(4, 8):
             project(ct)
         to_mu(2)
         to_mu(3)
         nc.vector.tensor_scalar(out=late_one[:], in0=st_[NB - 1][:, 0, 0:1], scalar1=0.0, scalar2=1.0,
                                 op0=ALU.mult, op1=ALU.add)
-        for b in range(NB):
-            product_q(b)
-            pair_sums(b, dt_[b], shalf, False, False)
+        for b0 in (0, 2):
+            product_q1(b0)
+            product_q1(b0 + 1)
+            product_q2(b0)
+            product_q2(b0 + 1)
+            pair_sums(b0, dt_[b0], shalf, True, False)
+            pair_sums(b0 + 1, dt_[b0 + 1], shalf, True, False)
         for b in range(NB):
             logs(b)
             turn_var_scale(b)

@@ -64,23 +64,22 @@ def tile_chainlveg_pa_kernel(tc, x, s_weight, s_mu, s_var, tcm_w, tcm_b,
         rawm = {}
         xs = keep.tile([P, NA, KD], BF16, name="xs")
 
-        def load_w(nm, q, gs=(0, 1)):
+        def load_v(g):
+            t = keep.tile([P, 4, NCH], U8, name="vbytes%d" % g)
+            vbytes[g] = t
+            nc.sync.dma_start(out=t[:], in_=tcv_w_bytes[512 * g:512 * (g + 1), :].rearrange("(p j) n -> p j n", j=4))
+
+        def load_m(q, g):
             c0, cw = CHUNKS[q]
-            for g in gs:
-                if nm == "v":
-                    t = keep.tile([P, 4, cw], U8, name="vbytes%d%d" % (g, q))
-                    src = tcv_w_bytes
-                    vbytes[(g, q)] = t
-                else:
-                    t = keep.tile([P, 4, cw], BF16, name="rawm%d%d" % (g, q))
-                    src = tcm_w
-                    rawm[(g, q)] = t
-                nc.sync.dma_start(out=t[:], in_=src[512 * g:512 * (g + 1), c0:c0 + cw].rearrange("(p j) n -> p j n", j=4))
+            t = keep.tile([P, 4, cw], BF16, name="rawm%d%d" % (g, q))
+            rawm[(g, q)] = t
+            nc.sync.dma_start(out=t[:], in_=tcm_w[512 * g:512 * (g + 1), c0:c0 + cw].rearrange("(p j) n -> p j n", j=4))
 
         nc.sync.dma_start(out=vsc[:], in_=tcv_w_scale.rearrange("(g p t) o -> p g (t o)", p=P, t=4))
-        load_w("m", 0, (0,))
-        load_w("v", 0)
-        load_w("m", 0, (1,))
+        load_m(0, 0)
+        load_v(0)
+        load_m(0, 1)
+        load_v(1)
         for a in range(NA):
             nc.sync.dma_start(out=xs[:, a, :], in_=xv[:, a, :])
         nc.sync.dma_start(out=brow[0:8, :], in_=tcm_b.rearrange("(c q) -> c q", q=P))
@@ -88,8 +87,8 @@ def tile_chainlveg_pa_kernel(tc, x, s_weight, s_mu, s_var, tcm_w, tcm_b,
         nc.sync.dma_start(out=sv[:], in_=svv)
         nc.sync.dma_start(out=sm[:], in_=smv)
         nc.sync.dma_start(out=sw[:], in_=swv)
-        load_w("m", 1)
-        load_w("v", 1)
+        load_m(1, 0)
+        load_m(1, 1)
 
         ident = keep.tile([P, P], F32, name="ident")
         make_identity(nc, ident[:])
@@ -167,11 +166,11 @@ def tile_chainlveg_pa_kernel(tc, x, s_weight, s_mu, s_var, tcm_w, tcm_b,
         grouped = {}
 
         def widen(q):
-            cw = CHUNKS[q][1]
+            c0, cw = CHUNKS[q]
             for g in range(NG):
                 t = keep.tile([P, 4, cw], BF16, name="wide%d%d" % (g, q))
                 for j in range(4):
-                    nc.scalar.activation(out=t[:, j, :], in_=vbytes[(g, q)][:, j, :].bitcast(FP8),
+                    nc.scalar.activation(out=t[:, j, :], in_=vbytes[g][:, j, c0:c0 + cw].bitcast(FP8),
                                          func=AF.Copy, scale=vsc[:, g, j:j + 1])
                 wide[(g, q)] = t
 
@@ -180,7 +179,8 @@ def tile_chainlveg_pa_kernel(tc, x, s_weight, s_mu, s_var, tcm_w, tcm_b,
             for g in range(NG):
                 src = rawm[(g, q)] if nm == "m" else wide[(g, q)]
                 t = keep.tile([P, cw, 4], BF16, name="grp%s%d%d" % (nm, g, q), align_bytes=64)
-                nc.vector.tensor_copy(out=t[:], in_=src[:].rearrange("p j n -> p n j"))
+                nc.vector.tensor_copy(out=t[:].rearrange("p (c i) j -> p c j i", i=4),
+                                      in_=src[:].rearrange("p j (c i) -> p c j i", i=4))
                 grouped[(nm, g, q)] = t
 
         def quantize_w(nm, q):

@@ -26,6 +26,8 @@ FLOPS = 2 * TOK * KD * 2 * NCH
 
 TOKEN_WINDOWS = ((0, 256), (256, 128))
 CHUNKS = ((0, 512), (512, 512))
+VAR_ON_VECTOR = (2, 3)
+VAR_BANK = (0, 0, 4, 6)
 SPOTS = [(a, c2) for a in range(NA) for c2 in range(2)]
 
 
@@ -45,9 +47,10 @@ def tile_chainlveg_pa_kernel(tc, x, s_weight, s_mu, s_var, tcm_w, tcm_b,
         keep = ctx.enter_context(tc.tile_pool(name="keep", bufs=1))
         front = ctx.enter_context(tc.tile_pool(name="front", bufs=NB))
         stage = ctx.enter_context(tc.tile_pool(name="stage", bufs=3))
-        pmx = ctx.enter_context(tc.psum_pool(name="pmx", bufs=1))
-        ptr = ctx.enter_context(tc.psum_pool(name="ptr", bufs=2))
-        psm = ctx.enter_context(tc.psum_pool(name="psm", bufs=4))
+        psum = ctx.enter_context(tc.psum_pool(name="psum", bufs=1))
+
+        def psum_bank(k, shape, dtype, label):
+            return psum.tile(shape, dtype, name=label, tag="bank%d" % k)
 
         sv = keep.tile([P, NA, 32], BF16, name="sv")
         sm = keep.tile([P, NA, 32], BF16, name="sm")
@@ -108,11 +111,13 @@ def tile_chainlveg_pa_kernel(tc, x, s_weight, s_mu, s_var, tcm_w, tcm_b,
         v1p = keep.tile([P, TOK], F32, name="v1p")
         m1p = keep.tile([P, TOK], F32, name="m1p")
         nie1 = keep.tile([P, TOK], F32, name="nie1")
+        v1d = keep.tile([P, TOK], F32, name="v1d")
+        v1x4 = keep.tile([P, NA, 4, 64], F32, name="v1x4")
         sg = keep.tile([P, 96], F32, name="sg")
         sgc = keep.tile([P, 96], F32, name="sgc")
 
         def bias_columns():
-            bt = ptr.tile([P, P], BF16, name="bt", tag="tr")
+            bt = psum_bank(7, [P, P], BF16, "bt")
             nc.tensor.transpose(bt[:], brow[:], identb[:])
             nc.vector.tensor_scalar(out=bias1[:], in0=bt[:, 0:16], scalar1=1.0, scalar2=None, op0=ALU.add)
 
@@ -121,11 +126,11 @@ def tile_chainlveg_pa_kernel(tc, x, s_weight, s_mu, s_var, tcm_w, tcm_b,
                 out=dst[:].rearrange("p a (j t g) -> p (a j) t g", t=2, g=2),
                 in_=src2.unsqueeze(2).to_broadcast([P, 48, 2, 2]))
 
-        def turned_table(label, dst, src, mul, add):
+        def turned_table(label, dst, src, mul, add, k):
             big = keep.tile([P, NA, 2, 64], F32, name="big" + label)
             nc.scalar.activation(out=big[:], in_=src[:].unsqueeze(2).to_broadcast([P, NA, 2, 64]), func=AF.Copy,
                                  scale=mul, bias=add)
-            tq = psm.tile([P, TOK], F32, name="tq", tag="sums")
+            tq = psum_bank(k, [P, TOK], F32, "tq")
             for a in range(NA):
                 nc.tensor.transpose(tq[:, a * P:(a + 1) * P], big[:, a, :, :].rearrange("p i c -> p (i c)"), ident[:])
             nc.scalar.copy(out=dst[:], in_=tq[:])
@@ -135,9 +140,9 @@ def tile_chainlveg_pa_kernel(tc, x, s_weight, s_mu, s_var, tcm_w, tcm_b,
             nc.scalar.activation(out=sg[:], in_=sv_flat, func=AF.Sigmoid, scale=-2.0)
             nc.scalar.activation(out=sgc[:], in_=sv_flat, func=AF.Sigmoid, scale=2.0)
             spread_t(v1x, sv[:].rearrange("p a (j g) -> p (a j) g", g=2))
-            turned_table("v1p", v1p, v1x, 1.0, 1.0)
+            turned_table("v1p", v1p, v1x, 1.0, 1.0, 4)
             spread_t(m1x, sm[:].rearrange("p a (j g) -> p (a j) g", g=2))
-            turned_table("m1p", m1p, m1x, 1.0, 1.0)
+            turned_table("m1p", m1p, m1x, 1.0, 1.0, 5)
 
         def tables_late():
             rc = keep.tile([P, 96], F32, name="rc")
@@ -145,7 +150,8 @@ def tile_chainlveg_pa_kernel(tc, x, s_weight, s_mu, s_var, tcm_w, tcm_b,
             nie = keep.tile([P, 96], F32, name="nie")
             nc.vector.scalar_tensor_tensor(out=nie[:], in0=sg[:], scalar=-1.0, in1=rc[:], op0=ALU.mult, op1=ALU.mult)
             spread_t(nex, nie[:].rearrange("p (c g) -> p c g", g=2))
-            turned_table("nie1", nie1, nex, 1.0, 0.0)
+            turned_table("nie1", nie1, nex, 1.0, 0.0, 6)
+            turned_table("v1d", v1d, v1x, 2.0, 2.0, 7)
             nc.vector.tensor_copy(out=v1x4[:], in_=v1x[:].unsqueeze(2).to_broadcast([P, NA, 4, 64]))
             svp = sv[:].rearrange("p a (j g) -> p (a j) g", g=2)
             vsum = keep.tile([P, 48], F32, name="vsum")
@@ -197,7 +203,7 @@ def tile_chainlveg_pa_kernel(tc, x, s_weight, s_mu, s_var, tcm_w, tcm_b,
         def turn_x():
             for a in range(NA):
                 words = xs[:, a, :].bitcast(F32)
-                xt = ptr.tile([P, NG, 2, P], F32, name="xt", tag="tr")
+                xt = psum_bank(4 + a, [P, NG, 2, P], F32, "xt")
                 for g in range(NG):
                     for u in range(2):
                         nc.tensor.transpose(xt[:, g, u, :], words[:, 256 * g + u:256 * (g + 1):2], ident[:])
@@ -221,8 +227,8 @@ def tile_chainlveg_pa_kernel(tc, x, s_weight, s_mu, s_var, tcm_w, tcm_b,
                 dt_[b] = front.tile([P, 2, TOK], F32, name="dd", tag="dd")
                 zt_[b] = front.tile([P, 2, TOK], F32, name="zz", tag="zz")
             cols = slice(ct * P, (ct + 1) * P)
-            for nm, tg, dst, bcol in (("v", "pv", zt_[b], 8 + ct), ("m", "pm", dt_[b], ct)):
-                acc = pmx.tile([P, TOK], F32, name="acc" + nm, tag=tg)
+            for nm, k, dst, bcol in (("v", (2 * ct) % 4, zt_[b], 8 + ct), ("m", (2 * ct + 1) % 4, dt_[b], ct)):
+                acc = psum_bank(k, [P, TOK], F32, "acc" + nm)
                 for t0, tw in TOKEN_WINDOWS:
                     for g in range(NG):
                         nc.tensor.matmul_mx(out=acc[:, t0:t0 + tw],
@@ -254,15 +260,9 @@ def tile_chainlveg_pa_kernel(tc, x, s_weight, s_mu, s_var, tcm_w, tcm_b,
         def product_q2(b):
             nc.vector.tensor_tensor(out=dt_[b][:], in0=dt_[b][:], in1=both(nie1), op=ALU.mult)
 
-        v1x4 = keep.tile([P, NA, 4, 64], F32, name="v1x4")
-
-        def turn_back(src, table, spare):
-            if spare:
-                lo = pmx.tile([P, 2, 256], F32, name="lo2", tag="pm")
-                hi = pmx.tile([P, 256], F32, name="hi2", tag="pv")
-            else:
-                lo = ptr.tile([P, 2, 256], F32, name="lo", tag="tr")
-                hi = ptr.tile([P, 256], F32, name="hi", tag="tr")
+        def turn_back(src, table, k):
+            lo = psum_bank(k, [P, 2, 256], F32, "lo")
+            hi = psum_bank(k + 1, [P, 256], F32, "hi")
             for bank, tiles in ((lo, (0, 1)), (hi, (2,))):
                 spots = [(a, c2) for a in tiles for c2 in range(2)]
                 if table is not None:
@@ -277,7 +277,7 @@ def tile_chainlveg_pa_kernel(tc, x, s_weight, s_mu, s_var, tcm_w, tcm_b,
             return lo, hi
 
         def turn_mu(b):
-            banks[("mu", b)] = turn_back(wt_[b], m1p, False)
+            banks[("mu", b)] = turn_back(wt_[b], m1p, 4 + 2 * (b % 2))
 
         def store_mu(b):
             lo, hi = banks[("mu", b)]
@@ -292,26 +292,30 @@ def tile_chainlveg_pa_kernel(tc, x, s_weight, s_mu, s_var, tcm_w, tcm_b,
 
         def pair_sums(b, src, mat, first, last):
             if first:
-                banks[("sc", b)] = psm.tile([P, NA, P], F32, name="sums", tag="sums")
+                banks[("sc", b)] = psum_bank(2 + b % 2, [P, NA, P], F32, "sums")
             sums = banks[("sc", b)]
             for k, (a, c2) in enumerate(SPOTS):
                 nc.tensor.matmul(out=sums[:, a, c2 * 64:(c2 + 1) * 64], lhsT=src[:, c2, a * P:(a + 1) * P], rhs=mat[:],
                                  start=(first and k == 0), stop=(last and k == len(SPOTS) - 1))
 
         def turn_var_scale(b):
-            banks[("var", b)] = turn_back(st_[b], None, b % 2 == 1)
+            banks[("var", b)] = turn_back(st_[b], None if b in VAR_ON_VECTOR else v1d, VAR_BANK[b])
             pair_sums(b, zt_[b], shalf, False, True)
 
         def store_var_scale(b):
             lo, hi = banks[("var", b)]
             res = stage.tile([P, NA, 256], F32, name="var", tag="var")
-            nc.vector.scalar_tensor_tensor(out=res[:, 0:2, :].rearrange("p a c -> p (a c)"),
-                                           in0=lo[:].rearrange("p a c -> p (a c)"), scalar=0.5,
-                                           in1=v1x4[:, 0:2, :, :].rearrange("p a i c -> p (a i c)"),
-                                           op0=ALU.mult, op1=ALU.add)
-            nc.vector.scalar_tensor_tensor(out=res[:, 2, :], in0=hi[:], scalar=0.5,
-                                           in1=v1x4[:, 2, :, :].rearrange("p i c -> p (i c)"),
-                                           op0=ALU.mult, op1=ALU.add)
+            if b in VAR_ON_VECTOR:
+                nc.vector.scalar_tensor_tensor(out=res[:, 0:2, :].rearrange("p a c -> p (a c)"),
+                                               in0=lo[:].rearrange("p a c -> p (a c)"), scalar=0.5,
+                                               in1=v1x4[:, 0:2, :, :].rearrange("p a i c -> p (a i c)"),
+                                               op0=ALU.mult, op1=ALU.add)
+                nc.vector.scalar_tensor_tensor(out=res[:, 2, :], in0=hi[:], scalar=0.5,
+                                               in1=v1x4[:, 2, :, :].rearrange("p i c -> p (i c)"),
+                                               op0=ALU.mult, op1=ALU.add)
+            else:
+                nc.scalar.activation(out=res[:, 0:2, :], in_=lo[:], func=AF.Copy, bias=-1.0, scale=0.5)
+                nc.scalar.activation(out=res[:, 2, :], in_=hi[:], func=AF.Copy, bias=-1.0, scale=0.5)
             nc.sync.dma_start(out=o2[:, :, 256 * b:256 * (b + 1)], in_=res[:])
             sums = banks[("sc", b)]
             res0 = stage.tile([P, NA, P], F32, name="sc", tag="sc")
@@ -345,24 +349,30 @@ def tile_chainlveg_pa_kernel(tc, x, s_weight, s_mu, s_var, tcm_w, tcm_b,
         widen(1)
         for ct in range(4):
             project(ct)
-        to_mu(0)
-        to_mu(1)
-        tables_late()
+        for b in range(2):
+            differences(b)
+            sigmoid(b)
         prepare(1)
         for ct in range(4, 8):
             project(ct)
-        to_mu(2)
-        to_mu(3)
+        for b in range(2, 4):
+            differences(b)
+            sigmoid(b)
         nc.vector.tensor_scalar(out=late_one[:], in0=st_[NB - 1][:, 0, 0:1], scalar1=0.0, scalar2=1.0,
                                 op0=ALU.mult, op1=ALU.add)
+        tables_late()
+        for b in range(NB):
+            product_w(b)
+        for b in range(NB):
+            logs(b)
+            turn_mu(b)
+            store_mu(b)
         for b0 in (0, 2):
             product_q1(b0)
             product_q1(b0 + 1)
             product_q2(b0)
             product_q2(b0 + 1)
-            pair_sums(b0, dt_[b0], shalf, True, False)
-            pair_sums(b0 + 1, dt_[b0 + 1], shalf, True, False)
         for b in range(NB):
-            logs(b)
+            pair_sums(b, dt_[b], shalf, True, False)
             turn_var_scale(b)
             store_var_scale(b)

@@ -26,8 +26,6 @@ FLOPS = 2 * TOK * KD * 2 * NCH
 
 TOKEN_WINDOWS = ((0, 256), (256, 128))
 CHUNKS = ((0, 512), (512, 512))
-VAR_ON_VECTOR = (2, 3)
-VAR_BANK = (0, 0, 4, 6)
 SPOTS = [(a, c2) for a in range(NA) for c2 in range(2)]
 
 
@@ -47,10 +45,9 @@ def tile_chainlveg_pa_kernel(tc, x, s_weight, s_mu, s_var, tcm_w, tcm_b,
         keep = ctx.enter_context(tc.tile_pool(name="keep", bufs=1))
         front = ctx.enter_context(tc.tile_pool(name="front", bufs=NB))
         stage = ctx.enter_context(tc.tile_pool(name="stage", bufs=3))
-        psum = ctx.enter_context(tc.psum_pool(name="psum", bufs=1))
-
-        def psum_bank(k, shape, dtype, label):
-            return psum.tile(shape, dtype, name=label, tag="bank%d" % k)
+        pmx = ctx.enter_context(tc.psum_pool(name="pmx", bufs=1))
+        ptr = ctx.enter_context(tc.psum_pool(name="ptr", bufs=2))
+        psm = ctx.enter_context(tc.psum_pool(name="psm", bufs=4))
 
         sv = keep.tile([P, NA, 32], BF16, name="sv")
         sm = keep.tile([P, NA, 32], BF16, name="sm")
@@ -111,13 +108,11 @@ def tile_chainlveg_pa_kernel(tc, x, s_weight, s_mu, s_var, tcm_w, tcm_b,
         v1p = keep.tile([P, TOK], F32, name="v1p")
         m1p = keep.tile([P, TOK], F32, name="m1p")
         nie1 = keep.tile([P, TOK], F32, name="nie1")
-        v1d = keep.tile([P, TOK], F32, name="v1d")
-        v1x4 = keep.tile([P, NA, 4, 64], F32, name="v1x4")
         sg = keep.tile([P, 96], F32, name="sg")
         sgc = keep.tile([P, 96], F32, name="sgc")
 
         def bias_columns():
-            bt = psum_bank(7, [P, P], BF16, "bt")
+            bt = ptr.tile([P, P], BF16, name="bt", tag="tr")
             nc.tensor.transpose(bt[:], brow[:], identb[:])
             nc.vector.tensor_scalar(out=bias1[:], in0=bt[:, 0:16], scalar1=1.0, scalar2=None, op0=ALU.add)
 
@@ -126,11 +121,11 @@ def tile_chainlveg_pa_kernel(tc, x, s_weight, s_mu, s_var, tcm_w, tcm_b,
                 out=dst[:].rearrange("p a (j t g) -> p (a j) t g", t=2, g=2),
                 in_=src2.unsqueeze(2).to_broadcast([P, 48, 2, 2]))
 
-        def turned_table(label, dst, src, mul, add, k):
+        def turned_table(label, dst, src, mul, add):
             big = keep.tile([P, NA, 2, 64], F32, name="big" + label)
             nc.scalar.activation(out=big[:], in_=src[:].unsqueeze(2).to_broadcast([P, NA, 2, 64]), func=AF.Copy,
                                  scale=mul, bias=add)
-            tq = psum_bank(k, [P, TOK], F32, "tq")
+            tq = psm.tile([P, TOK], F32, name="tq", tag="sums")
             for a in range(NA):
                 nc.tensor.transpose(tq[:, a * P:(a + 1) * P], big[:, a, :, :].rearrange("p i c -> p (i c)"), ident[:])
             nc.scalar.copy(out=dst[:], in_=tq[:])
@@ -140,9 +135,9 @@ def tile_chainlveg_pa_kernel(tc, x, s_weight, s_mu, s_var, tcm_w, tcm_b,
             nc.scalar.activation(out=sg[:], in_=sv_flat, func=AF.Sigmoid, scale=-2.0)
             nc.scalar.activation(out=sgc[:], in_=sv_flat, func=AF.Sigmoid, scale=2.0)
             spread_t(v1x, sv[:].rearrange("p a (j g) -> p (a j) g", g=2))
-            turned_table("v1p", v1p, v1x, 1.0, 1.0, 4)
+            turned_table("v1p", v1p, v1x, 1.0, 1.0)
             spread_t(m1x, sm[:].rearrange("p a (j g) -> p (a j) g", g=2))
-            turned_table("m1p", m1p, m1x, 1.0, 1.0, 5)
+            turned_table("m1p", m1p, m1x, 1.0, 1.0)
 
         def tables_late():
             rc = keep.tile([P, 96], F32, name="rc")
@@ -150,8 +145,7 @@ def tile_chainlveg_pa_kernel(tc, x, s_weight, s_mu, s_var, tcm_w, tcm_b,
             nie = keep.tile([P, 96], F32, name="nie")
             nc.vector.scalar_tensor_tensor(out=nie[:], in0=sg[:], scalar=-1.0, in1=rc[:], op0=ALU.mult, op1=ALU.mult)
             spread_t(nex, nie[:].rearrange("p (c g) -> p c g", g=2))
-            turned_table("nie1", nie1, nex, 1.0, 0.0, 6)
-            turned_table("v1d", v1d, v1x, 2.0, 2.0, 7)
+            turned_table("nie1", nie1, nex, 1.0, 0.0)
             nc.vector.tensor_copy(out=v1x4[:], in_=v1x[:].unsqueeze(2).to_broadcast([P, NA, 4, 64]))
             svp = sv[:].rearrange("p a (j g) -> p (a j) g", g=2)
             vsum = keep.tile([P, 48], F32, name="vsum")
@@ -203,7 +197,7 @@ def tile_chainlveg_pa_kernel(tc, x, s_weight, s_mu, s_var, tcm_w, tcm_b,
         def turn_x():
             for a in range(NA):
                 words = xs[:, a, :].bitcast(F32)
-                xt = psum_bank(4 + a, [P, NG, 2, P], F32, "xt")
+                xt = ptr.tile([P, NG, 2, P], F32, name="xt", tag="tr")
                 for g in range(NG):
                     for u in range(2):
                         nc.tensor.transpose(xt[:, g, u, :], words[:, 256 * g + u:256 * (g + 1):2], ident[:])
@@ -227,8 +221,8 @@ def tile_chainlveg_pa_kernel(tc, x, s_weight, s_mu, s_var, tcm_w, tcm_b,
                 dt_[b] = front.tile([P, 2, TOK], F32, name="dd", tag="dd")
                 zt_[b] = front.tile([P, 2, TOK], F32, name="zz", tag="zz")
             cols = slice(ct * P, (ct + 1) * P)
-            for nm, k, dst, bcol in (("v", (2 * ct) % 4, zt_[b], 8 + ct), ("m", (2 * ct + 1) % 4, dt_[b], ct)):
-                acc = psum_bank(k, [P, TOK], F32, "acc" + nm)
+            for nm, tg, dst, bcol in (("v", "pv", zt_[b], 8 + ct), ("m", "pm", dt_[b], ct)):
+                acc = pmx.tile([P, TOK], F32, name="acc" + nm, tag=tg)
                 for t0, tw in TOKEN_WINDOWS:
                     for g in range(NG):
                         nc.tensor.matmul_mx(out=acc[:, t0:t0 + tw],
@@ -260,9 +254,15 @@ def tile_chainlveg_pa_kernel(tc, x, s_weight, s_mu, s_var, tcm_w, tcm_b,
         def product_q2(b):
             nc.vector.tensor_tensor(out=dt_[b][:], in0=dt_[b][:], in1=both(nie1), op=ALU.mult)
 
-        def turn_back(src, table, k):
-            lo = psum_bank(k, [P, 2, 256], F32, "lo")
-            hi = psum_bank(k + 1, [P, 256], F32, "hi")
+        v1x4 = keep.tile([P, NA, 4, 64], F32, name="v1x4")
+
+        def turn_back(src, table, spare):
+            if spare:
+                lo = pmx.tile([P, 2, 256], F32, name="lo2", tag="pm")
+                hi = pmx.tile([P, 256], F32, name="hi2", tag="pv")
+            else:
+                lo = ptr.tile([P, 2, 256], F32, name="lo", tag="tr")
+                hi = ptr.tile([P, 256], F32, name="hi", tag="tr")
             for bank, tiles in ((lo, (0, 1)), (hi, (2,))):
                 spots = [(a, c2) for a in tiles for c2 in range(2)]
                 if table is not None:
@@ -277,14 +277,15 @@ def tile_chainlveg_pa_kernel(tc, x, s_weight, s_mu, s_var, tcm_w, tcm_b,
             return lo, hi
 
         def turn_mu(b):
-            banks[("mu", b)] = turn_back(wt_[b], m1p, 4 + 2 * (b % 2))
+            banks[("mu", b)] = turn_back(wt_[b], m1p, False)
 
         def store_mu(b):
             lo, hi = banks[("mu", b)]
             res = stage.tile([P, NA, 256], F32, name="mu", tag="mu")
             nc.scalar.activation(out=res[:, 0:2, :], in_=lo[:], func=AF.Copy, bias=-1.0, scale=1.0)
+            nc.sync.dma_start(out=o1[:, 0:2, 256 * b:256 * (b + 1)], in_=res[:, 0:2, :])
             nc.scalar.activation(out=res[:, 2, :], in_=hi[:], func=AF.Copy, bias=-1.0, scale=1.0)
-            nc.sync.dma_start(out=o1[:, :, 256 * b:256 * (b + 1)], in_=res[:])
+            nc.sync.dma_start(out=o1[:, 2, 256 * b:256 * (b + 1)], in_=res[:, 2, :])
 
         def logs(b):
             nc.scalar.activation(out=zt_[b][:], in_=st_[b][:], func=AF.Ln, scale=late_one[:, 0:1])
@@ -292,31 +293,28 @@ def tile_chainlveg_pa_kernel(tc, x, s_weight, s_mu, s_var, tcm_w, tcm_b,
 
         def pair_sums(b, src, mat, first, last):
             if first:
-                banks[("sc", b)] = psum_bank(2 + b % 2, [P, NA, P], F32, "sums")
+                banks[("sc", b)] = psm.tile([P, NA, P], F32, name="sums", tag="sums")
             sums = banks[("sc", b)]
             for k, (a, c2) in enumerate(SPOTS):
                 nc.tensor.matmul(out=sums[:, a, c2 * 64:(c2 + 1) * 64], lhsT=src[:, c2, a * P:(a + 1) * P], rhs=mat[:],
                                  start=(first and k == 0), stop=(last and k == len(SPOTS) - 1))
 
         def turn_var_scale(b):
-            banks[("var", b)] = turn_back(st_[b], None if b in VAR_ON_VECTOR else v1d, VAR_BANK[b])
+            banks[("var", b)] = turn_back(st_[b], None, b % 2 == 1)
             pair_sums(b, zt_[b], shalf, False, True)
 
         def store_var_scale(b):
             lo, hi = banks[("var", b)]
             res = stage.tile([P, NA, 256], F32, name="var", tag="var")
-            if b in VAR_ON_VECTOR:
-                nc.vector.scalar_tensor_tensor(out=res[:, 0:2, :].rearrange("p a c -> p (a c)"),
-                                               in0=lo[:].rearrange("p a c -> p (a c)"), scalar=0.5,
-                                               in1=v1x4[:, 0:2, :, :].rearrange("p a i c -> p (a i c)"),
-                                               op0=ALU.mult, op1=ALU.add)
-                nc.vector.scalar_tensor_tensor(out=res[:, 2, :], in0=hi[:], scalar=0.5,
-                                               in1=v1x4[:, 2, :, :].rearrange("p i c -> p (i c)"),
-                                               op0=ALU.mult, op1=ALU.add)
-            else:
-                nc.scalar.activation(out=res[:, 0:2, :], in_=lo[:], func=AF.Copy, bias=-1.0, scale=0.5)
-                nc.scalar.activation(out=res[:, 2, :], in_=hi[:], func=AF.Copy, bias=-1.0, scale=0.5)
-            nc.sync.dma_start(out=o2[:, :, 256 * b:256 * (b + 1)], in_=res[:])
+            nc.vector.scalar_tensor_tensor(out=res[:, 0:2, :].rearrange("p a c -> p (a c)"),
+                                           in0=lo[:].rearrange("p a c -> p (a c)"), scalar=0.5,
+                                           in1=v1x4[:, 0:2, :, :].rearrange("p a i c -> p (a i c)"),
+                                           op0=ALU.mult, op1=ALU.add)
+            nc.sync.dma_start(out=o2[:, 0:2, 256 * b:256 * (b + 1)], in_=res[:, 0:2, :])
+            nc.vector.scalar_tensor_tensor(out=res[:, 2, :], in0=hi[:], scalar=0.5,
+                                           in1=v1x4[:, 2, :, :].rearrange("p i c -> p (i c)"),
+                                           op0=ALU.mult, op1=ALU.add)
+            nc.sync.dma_start(out=o2[:, 2, 256 * b:256 * (b + 1)], in_=res[:, 2, :])
             sums = banks[("sc", b)]
             res0 = stage.tile([P, NA, P], F32, name="sc", tag="sc")
             nc.vector.tensor_tensor(out=res0[:].rearrange("p a (i c) -> p a i c", i=4),
@@ -349,30 +347,23 @@ def tile_chainlveg_pa_kernel(tc, x, s_weight, s_mu, s_var, tcm_w, tcm_b,
         widen(1)
         for ct in range(4):
             project(ct)
-        for b in range(2):
-            differences(b)
-            sigmoid(b)
+        to_mu(0)
+        to_mu(1)
+        tables_late()
         prepare(1)
         for ct in range(4, 8):
             project(ct)
-        for b in range(2, 4):
-            differences(b)
-            sigmoid(b)
-        nc.vector.tensor_scalar(out=late_one[:], in0=st_[NB - 1][:, 0, 0:1], scalar1=0.0, scalar2=1.0,
-                                op0=ALU.mult, op1=ALU.add)
-        tables_late()
-        for b in range(NB):
-            product_w(b)
-        for b in range(NB):
-            logs(b)
-            turn_mu(b)
-            store_mu(b)
+        to_mu(2)
+        to_mu(3)
+        nc.scalar.activation(out=late_one[:], in_=st_[NB - 1][:, 0, 0:1], func=AF.Copy, scale=0.0, bias=1.0)
         for b0 in (0, 2):
             product_q1(b0)
             product_q1(b0 + 1)
             product_q2(b0)
             product_q2(b0 + 1)
+            pair_sums(b0, dt_[b0], shalf, True, False)
+            pair_sums(b0 + 1, dt_[b0 + 1], shalf, True, False)
         for b in range(NB):
-            pair_sums(b, dt_[b], shalf, True, False)
+            logs(b)
             turn_var_scale(b)
             store_var_scale(b)

@@ -19,14 +19,13 @@ NA = 3
 KD = 1024
 NG = 2
 NCH = 1024
-NB = 4
+NQ = 2
+CW = 512
 LOG_2PI = math.log(2.0 * math.pi)
 
 FLOPS = 2 * TOK * KD * 2 * NCH
 
 TOKEN_WINDOWS = ((0, 256), (256, 128))
-CHUNKS = ((0, 512), (512, 512))
-SPOTS = [(a, c2) for a in range(NA) for c2 in range(2)]
 
 
 def tile_chainlveg_pa_kernel(tc, x, s_weight, s_mu, s_var, tcm_w, tcm_b,
@@ -43,7 +42,6 @@ def tile_chainlveg_pa_kernel(tc, x, s_weight, s_mu, s_var, tcm_w, tcm_b,
 
     with ExitStack() as ctx:
         keep = ctx.enter_context(tc.tile_pool(name="keep", bufs=1))
-        front = ctx.enter_context(tc.tile_pool(name="front", bufs=NB))
         stage = ctx.enter_context(tc.tile_pool(name="stage", bufs=3))
         pmx = ctx.enter_context(tc.psum_pool(name="pmx", bufs=1))
         ptr = ctx.enter_context(tc.psum_pool(name="ptr", bufs=2))
@@ -53,7 +51,7 @@ def tile_chainlveg_pa_kernel(tc, x, s_weight, s_mu, s_var, tcm_w, tcm_b,
         sm = keep.tile([P, NA, 32], BF16, name="sm")
         sw = keep.tile([P, NA, 16], BF16, name="sw")
         vsc = keep.tile([P, NG, 4], F32, name="vsc")
-        brow = keep.tile([P, P], BF16, name="brow")
+        brow = keep.tile([P, 256], BF16, name="brow")
         nc.vector.memset(brow[:], 0.0)
         warm = keep.tile([P, 1], F32, name="warm")
         nc.vector.memset(warm[:], 0.0)
@@ -70,22 +68,21 @@ def tile_chainlveg_pa_kernel(tc, x, s_weight, s_mu, s_var, tcm_w, tcm_b,
             nc.sync.dma_start(out=t[:], in_=tcv_w_bytes[512 * g:512 * (g + 1), :].rearrange("(p j) n -> p j n", j=4))
 
         def load_m(q, g):
-            c0, cw = CHUNKS[q]
-            t = keep.tile([P, 4, cw], BF16, name="rawm%d%d" % (g, q))
+            t = keep.tile([P, 4, CW], BF16, name="rawm%d%d" % (g, q))
             rawm[(g, q)] = t
-            nc.sync.dma_start(out=t[:], in_=tcm_w[512 * g:512 * (g + 1), c0:c0 + cw].rearrange("(p j) n -> p j n", j=4))
+            nc.sync.dma_start(out=t[:], in_=tcm_w[512 * g:512 * (g + 1), CW * q:CW * (q + 1)].rearrange("(p j) n -> p j n", j=4))
 
         nc.sync.dma_start(out=vsc[:], in_=tcv_w_scale.rearrange("(g p t) o -> p g (t o)", p=P, t=4))
+        nc.sync.dma_start(out=sv[:], in_=svv)
+        nc.sync.dma_start(out=sm[:], in_=smv)
         load_m(0, 0)
         load_v(0)
         load_m(0, 1)
         load_v(1)
         for a in range(NA):
             nc.sync.dma_start(out=xs[:, a, :], in_=xv[:, a, :])
-        nc.sync.dma_start(out=brow[0:8, :], in_=tcm_b.rearrange("(c q) -> c q", q=P))
-        nc.sync.dma_start(out=brow[8:16, :], in_=tcv_b.rearrange("(c q) -> c q", q=P))
-        nc.sync.dma_start(out=sv[:], in_=svv)
-        nc.sync.dma_start(out=sm[:], in_=smv)
+        nc.sync.dma_start(out=brow[0:4, :], in_=tcm_b.rearrange("(c q) -> c q", q=256))
+        nc.sync.dma_start(out=brow[4:8, :], in_=tcv_b.rearrange("(c q) -> c q", q=256))
         nc.sync.dma_start(out=sw[:], in_=swv)
         load_m(1, 0)
         load_m(1, 1)
@@ -95,58 +92,49 @@ def tile_chainlveg_pa_kernel(tc, x, s_weight, s_mu, s_var, tcm_w, tcm_b,
         identb = keep.tile([P, P], BF16, name="identb")
         make_identity(nc, identb[:])
         late_one = keep.tile([P, 1], F32, name="late_one")
-        pair = keep.tile([P, 64], F32, name="pair")
-        nc.vector.tensor_tensor(out=pair[:], in0=ident[:, 0:P:2], in1=ident[:, 1:P:2], op=ALU.add)
-        shalf = keep.tile([P, 64], F32, name="shalf")
-        nc.vector.tensor_scalar(out=shalf[:], in0=pair[:], scalar1=0.5, scalar2=None, op0=ALU.mult)
 
-        m1x = keep.tile([P, NA, 64], F32, name="m1x")
         v1x = keep.tile([P, NA, 64], F32, name="v1x")
-        nex = keep.tile([P, NA, 64], F32, name="nex")
         t0x = keep.tile([P, NA, 32], F32, name="t0x")
-        bias1 = keep.tile([P, 16], F32, name="bias1")
-        v1p = keep.tile([P, TOK], F32, name="v1p")
-        m1p = keep.tile([P, TOK], F32, name="m1p")
-        nie1 = keep.tile([P, TOK], F32, name="nie1")
+        biasm = keep.tile([P, 2, 4], F32, name="biasm")
+        biasv = keep.tile([P, 2, 4], F32, name="biasv")
+        tblv = keep.tile([P, 2, TOK], F32, name="tblv")
+        m1p = keep.tile([P, 2, TOK], F32, name="m1p")
+        nie1 = keep.tile([P, 2, TOK], F32, name="nie1")
         sg = keep.tile([P, 96], F32, name="sg")
         sgc = keep.tile([P, 96], F32, name="sgc")
 
         def bias_columns():
-            bt = ptr.tile([P, P], BF16, name="bt", tag="tr")
-            nc.tensor.transpose(bt[:], brow[:], identb[:])
-            nc.vector.tensor_scalar(out=bias1[:], in0=bt[:, 0:16], scalar1=1.0, scalar2=None, op0=ALU.add)
+            browg = keep.tile([P, 2, P], BF16, name="browg")
+            nc.vector.tensor_copy(out=browg[:], in_=brow[:].rearrange("p (m g) -> p g m", g=2))
+            bt = ptr.tile([P, 2, P], BF16, name="bt", tag="tr")
+            for g in range(2):
+                nc.tensor.transpose(bt[:, g, :], browg[:, g, :], identb[:])
+            nc.vector.tensor_scalar(out=biasm[:], in0=bt[:, :, 0:4], scalar1=1.0, scalar2=None, op0=ALU.add)
+            nc.vector.tensor_scalar(out=biasv[:], in0=bt[:, :, 4:8], scalar1=-2.0, scalar2=2.0, op0=ALU.mult, op1=ALU.add)
 
-        def spread_t(dst, src2):
+        bigs = {}
+
+        def table_lay(label, src3, mul, add):
+            y = keep.tile([P, NA, 2, 32], F32, name="y" + label)
+            nc.vector.tensor_copy(out=y[:].rearrange("p a g (j t) -> p a g j t", t=2),
+                                  in_=src3.rearrange("p a (j g) -> p a g j", g=2).unsqueeze(4).to_broadcast([P, NA, 2, 16, 2]))
+            big = keep.tile([P, NA * 2, 4, 32], F32, name="big" + label)
+            nc.vector.tensor_scalar(out=big[:], in0=y[:].rearrange("p a g c -> p (a g) c").unsqueeze(2).to_broadcast([P, NA * 2, 4, 32]),
+                                    scalar1=mul, scalar2=add, op0=ALU.mult, op1=ALU.add)
+            bigs[label] = big
+
+        def table_turn(label, dst):
+            big = bigs[label]
+            for g in range(2):
+                tq = psm.tile([P, TOK], F32, name="tq", tag="sums")
+                for a in range(NA):
+                    nc.tensor.transpose(tq[:, a * P:(a + 1) * P], big[:, a * 2 + g, :, :].rearrange("p i c -> p (i c)"), ident[:])
+                nc.scalar.copy(out=dst[:, g, :], in_=tq[:])
+
+        def tables_small():
             nc.vector.tensor_copy(
-                out=dst[:].rearrange("p a (j t g) -> p (a j) t g", t=2, g=2),
-                in_=src2.unsqueeze(2).to_broadcast([P, 48, 2, 2]))
-
-        def turned_table(label, dst, src, mul, add):
-            big = keep.tile([P, NA, 2, 64], F32, name="big" + label)
-            nc.scalar.activation(out=big[:], in_=src[:].unsqueeze(2).to_broadcast([P, NA, 2, 64]), func=AF.Copy,
-                                 scale=mul, bias=add)
-            tq = psm.tile([P, TOK], F32, name="tq", tag="sums")
-            for a in range(NA):
-                nc.tensor.transpose(tq[:, a * P:(a + 1) * P], big[:, a, :, :].rearrange("p i c -> p (i c)"), ident[:])
-            nc.scalar.copy(out=dst[:], in_=tq[:])
-
-        def tables():
-            sv_flat = sv[:].rearrange("p a c -> p (a c)")
-            nc.scalar.activation(out=sg[:], in_=sv_flat, func=AF.Sigmoid, scale=-2.0)
-            nc.scalar.activation(out=sgc[:], in_=sv_flat, func=AF.Sigmoid, scale=2.0)
-            spread_t(v1x, sv[:].rearrange("p a (j g) -> p (a j) g", g=2))
-            turned_table("v1p", v1p, v1x, 1.0, 1.0)
-            spread_t(m1x, sm[:].rearrange("p a (j g) -> p (a j) g", g=2))
-            turned_table("m1p", m1p, m1x, 1.0, 1.0)
-
-        def tables_late():
-            rc = keep.tile([P, 96], F32, name="rc")
-            nc.vector.reciprocal(out=rc[:], in_=sgc[:])
-            nie = keep.tile([P, 96], F32, name="nie")
-            nc.vector.scalar_tensor_tensor(out=nie[:], in0=sg[:], scalar=-1.0, in1=rc[:], op0=ALU.mult, op1=ALU.mult)
-            spread_t(nex, nie[:].rearrange("p (c g) -> p c g", g=2))
-            turned_table("nie1", nie1, nex, 1.0, 0.0)
-            nc.vector.tensor_copy(out=v1x4[:], in_=v1x[:].unsqueeze(2).to_broadcast([P, NA, 4, 64]))
+                out=v1x[:].rearrange("p a (j t g) -> p (a j) t g", t=2, g=2),
+                in_=sv[:].rearrange("p a (j g) -> p (a j) g", g=2).unsqueeze(2).to_broadcast([P, 48, 2, 2]))
             svp = sv[:].rearrange("p a (j g) -> p (a j) g", g=2)
             vsum = keep.tile([P, 48], F32, name="vsum")
             nc.vector.tensor_tensor(out=vsum[:], in0=svp[:, :, 0], in1=svp[:, :, 1], op=ALU.add)
@@ -157,6 +145,13 @@ def tile_chainlveg_pa_kernel(tc, x, s_weight, s_mu, s_var, tcm_w, tcm_b,
                 in1=vsum[:].unsqueeze(2).to_broadcast([P, 48, 2]),
                 op0=ALU.add, op1=ALU.subtract)
 
+        def nie_lay():
+            rc = keep.tile([P, 96], F32, name="rc")
+            nc.vector.reciprocal(out=rc[:], in_=sgc[:])
+            nie = keep.tile([P, 96], F32, name="nie")
+            nc.vector.scalar_tensor_tensor(out=nie[:], in0=sg[:], scalar=-1.0, in1=rc[:], op0=ALU.mult, op1=ALU.mult)
+            table_lay("n", nie[:].rearrange("p (a c) -> p a c", a=NA), 1.0, 0.0)
+
         wcod = {}
         wscl = {}
         for nm in ("m", "v"):
@@ -166,27 +161,24 @@ def tile_chainlveg_pa_kernel(tc, x, s_weight, s_mu, s_var, tcm_w, tcm_b,
         grouped = {}
 
         def widen(q):
-            c0, cw = CHUNKS[q]
             for g in range(NG):
-                t = keep.tile([P, 4, cw], BF16, name="wide%d%d" % (g, q))
+                t = keep.tile([P, 4, CW], BF16, name="wide%d%d" % (g, q))
                 for j in range(4):
-                    nc.scalar.activation(out=t[:, j, :], in_=vbytes[g][:, j, c0:c0 + cw].bitcast(FP8),
+                    nc.scalar.activation(out=t[:, j, :], in_=vbytes[g][:, j, CW * q:CW * (q + 1)].bitcast(FP8),
                                          func=AF.Copy, scale=vsc[:, g, j:j + 1])
                 wide[(g, q)] = t
 
         def interleave(nm, q):
-            cw = CHUNKS[q][1]
             for g in range(NG):
                 src = rawm[(g, q)] if nm == "m" else wide[(g, q)]
-                t = keep.tile([P, cw, 4], BF16, name="grp%s%d%d" % (nm, g, q), align_bytes=64)
-                nc.vector.tensor_copy(out=t[:].rearrange("p (c i) j -> p c j i", i=4),
-                                      in_=src[:].rearrange("p j (c i) -> p c j i", i=4))
+                t = keep.tile([P, CW, 4], BF16, name="grp%s%d%d" % (nm, g, q), align_bytes=64)
+                nc.vector.tensor_copy(out=t[:].rearrange("p (h c i) j -> p h c j i", h=2, i=4),
+                                      in_=src[:].rearrange("p j (c i h) -> p h c j i", i=4, h=2))
                 grouped[(nm, g, q)] = t
 
         def quantize_w(nm, q):
-            c0, cw = CHUNKS[q]
             for g in range(NG):
-                nc.vector.quantize_mx(out=wcod[nm][:, g, c0:c0 + cw].bitcast(FP8X4), scales=wscl[nm][:, g, c0:c0 + cw],
+                nc.vector.quantize_mx(out=wcod[nm][:, g, CW * q:CW * (q + 1)].bitcast(FP8X4), scales=wscl[nm][:, g, CW * q:CW * (q + 1)],
                                       in_=grouped[(nm, g, q)][:].rearrange("p n j -> p (n j)"))
 
         xg = keep.tile([P, NG, 4 * TOK], BF16, name="xg", align_bytes=64)
@@ -209,19 +201,22 @@ def tile_chainlveg_pa_kernel(tc, x, s_weight, s_mu, s_var, tcm_w, tcm_b,
                     nc.vector.quantize_mx(out=xcod[:, g, t0:t0 + tw].bitcast(FP8X4), scales=xscl[:, g, t0:t0 + tw],
                                           in_=xg[:, g, 4 * t0:4 * (t0 + tw)])
 
+        ut_ = {}
         dt_ = {}
-        zt_ = {}
         st_ = {}
         wt_ = {}
-        banks = {}
+        for q in range(NQ):
+            ut_[q] = keep.tile([P, 2, 2, TOK], F32, name="uu%d" % q)
+            dt_[q] = keep.tile([P, 2, 2, TOK], F32, name="dd%d" % q)
+            st_[q] = keep.tile([P, 2, 2, TOK], F32, name="ss%d" % q)
+            wt_[q] = keep.tile([P, 2, 2, TOK], F32, name="ww%d" % q)
+        sums = {}
 
-        def project(ct):
-            b, c2 = divmod(ct, 2)
-            if c2 == 0:
-                dt_[b] = front.tile([P, 2, TOK], F32, name="dd", tag="dd")
-                zt_[b] = front.tile([P, 2, TOK], F32, name="zz", tag="zz")
-            cols = slice(ct * P, (ct + 1) * P)
-            for nm, tg, dst, bcol in (("v", "pv", zt_[b], 8 + ct), ("m", "pm", dt_[b], ct)):
+        def project(q, bl, h):
+            c0 = CW * q + 256 * h + P * bl
+            cols = slice(c0, c0 + P)
+            blk = 2 * q + bl
+            for nm, tg, dst, bias, mul in (("v", "pv", ut_[q], biasv, -2.0), ("m", "pm", dt_[q], biasm, 1.0)):
                 acc = pmx.tile([P, TOK], F32, name="acc" + nm, tag=tg)
                 for t0, tw in TOKEN_WINDOWS:
                     for g in range(NG):
@@ -229,112 +224,114 @@ def tile_chainlveg_pa_kernel(tc, x, s_weight, s_mu, s_var, tcm_w, tcm_b,
                                             lhsT=wcod[nm][:, g, cols].bitcast(FP8X4), lhsT_scale=wscl[nm][:, g, cols],
                                             rhs=xcod[:, g, t0:t0 + tw].bitcast(FP8X4), rhs_scale=xscl[:, g, t0:t0 + tw],
                                             start=(g == 0), stop=(g == NG - 1))
-                nc.scalar.activation(out=dst[:, c2, :], in_=acc[:], func=AF.Relu, bias=bias1[:, bcol:bcol + 1], scale=1.0)
+                nc.scalar.activation(out=dst[:, bl, h, :], in_=acc[:], func=AF.Relu, bias=bias[:, h, blk:blk + 1], scale=mul)
 
-        def both(t):
-            return t[:].unsqueeze(1).to_broadcast([P, 2, TOK])
+        def flat(t, bl):
+            return t[:, bl, :, :].rearrange("p g t -> p (g t)")
 
-        def differences(b):
-            nc.vector.scalar_tensor_tensor(out=zt_[b][:], in0=zt_[b][:], scalar=2.0, in1=both(v1p),
+        def flat2(t):
+            return t[:].rearrange("p g t -> p (g t)")
+
+        def differences(q, bl):
+            nc.vector.scalar_tensor_tensor(out=flat(ut_[q], bl), in0=flat(ut_[q], bl), scalar=4.0, in1=flat2(tblv),
                                            op0=ALU.min, op1=ALU.subtract)
-            nc.vector.scalar_tensor_tensor(out=dt_[b][:], in0=dt_[b][:], scalar=2.0, in1=both(m1p),
+            nc.vector.scalar_tensor_tensor(out=flat(dt_[q], bl), in0=flat(dt_[q], bl), scalar=2.0, in1=flat2(m1p),
                                            op0=ALU.min, op1=ALU.subtract)
 
-        def sigmoid(b):
-            st_[b] = front.tile([P, 2, TOK], F32, name="ss", tag="ss")
-            nc.scalar.activation(out=st_[b][:], in_=zt_[b][:], func=AF.Sigmoid, scale=-2.0)
+        def sigmoid(q, bl):
+            nc.scalar.activation(out=flat(st_[q], bl), in_=flat(ut_[q], bl), func=AF.Sigmoid)
 
-        def product_w(b):
-            wt_[b] = front.tile([P, 2, TOK], F32, name="ww", tag="ww")
-            nc.vector.tensor_tensor(out=wt_[b][:], in0=dt_[b][:], in1=st_[b][:], op=ALU.mult)
+        def product_w(q, bl):
+            nc.vector.tensor_tensor(out=flat(wt_[q], bl), in0=flat(dt_[q], bl), in1=flat(st_[q], bl), op=ALU.mult)
 
-        def product_q1(b):
-            nc.vector.tensor_tensor(out=dt_[b][:], in0=wt_[b][:], in1=dt_[b][:], op=ALU.mult)
+        def product_q1(q, bl):
+            nc.vector.tensor_tensor(out=flat(dt_[q], bl), in0=flat(wt_[q], bl), in1=flat(dt_[q], bl), op=ALU.mult)
 
-        def product_q2(b):
-            nc.vector.tensor_tensor(out=dt_[b][:], in0=dt_[b][:], in1=both(nie1), op=ALU.mult)
+        def product_q2(q, bl):
+            nc.vector.tensor_tensor(out=flat(dt_[q], bl), in0=flat(dt_[q], bl), in1=flat2(nie1), op=ALU.mult)
 
-        v1x4 = keep.tile([P, NA, 4, 64], F32, name="v1x4")
+        def turned_bank(k):
+            if k % 2 == 0:
+                return ptr.tile([P, 2, 256], F32, name="tb", tag="tr")
+            return pmx.tile([P, 2, 256], F32, name="tb2", tag=("pm" if k % 4 == 1 else "pv"))
 
-        def turn_back(src, table, spare):
-            if spare:
-                lo = pmx.tile([P, 2, 256], F32, name="lo2", tag="pm")
-                hi = pmx.tile([P, 256], F32, name="hi2", tag="pv")
-            else:
-                lo = ptr.tile([P, 2, 256], F32, name="lo", tag="tr")
-                hi = ptr.tile([P, 256], F32, name="hi", tag="tr")
-            for bank, tiles in ((lo, (0, 1)), (hi, (2,))):
-                spots = [(a, c2) for a in tiles for c2 in range(2)]
-                if table is not None:
-                    for k, (a, c2) in enumerate(spots):
-                        dst = bank[:, a, c2 * P:(c2 + 1) * P] if a < 2 else bank[:, c2 * P:(c2 + 1) * P]
-                        nc.tensor.matmul(out=dst, lhsT=table[:, a * P:(a + 1) * P], rhs=ident[:], is_transpose=True,
-                                         start=(k == 0), stop=False)
-                for k, (a, c2) in enumerate(spots):
-                    dst = bank[:, a, c2 * P:(c2 + 1) * P] if a < 2 else bank[:, c2 * P:(c2 + 1) * P]
-                    nc.tensor.matmul(out=dst, lhsT=src[:, c2, a * P:(a + 1) * P], rhs=ident[:], is_transpose=True,
-                                     start=(table is None and k == 0), stop=(k == len(spots) - 1))
-            return lo, hi
+        def turn_unit(bank, src, a, table):
+            spots = [(h, bl) for h in range(2) for bl in range(2)]
+            tok = slice(a * P, (a + 1) * P)
+            if table is not None:
+                for k, (h, bl) in enumerate(spots):
+                    nc.tensor.matmul(out=bank[:, h, bl * P:(bl + 1) * P], lhsT=table[:, h, tok], rhs=ident[:], is_transpose=True,
+                                     start=(k == 0), stop=False)
+            for k, (h, bl) in enumerate(spots):
+                nc.tensor.matmul(out=bank[:, h, bl * P:(bl + 1) * P], lhsT=src[:, bl, h, tok], rhs=ident[:], is_transpose=True,
+                                 start=(table is None and k == 0), stop=(k == len(spots) - 1))
 
-        def turn_mu(b):
-            banks[("mu", b)] = turn_back(wt_[b], m1p, False)
+        def mu_unit(q, a):
+            bank = ptr.tile([P, 2, 256], F32, name="tb", tag="tr")
+            turn_unit(bank, wt_[q], a, m1p)
+            res = stage.tile([P, CW], F32, name="mu", tag="mu")
+            nc.scalar.activation(out=res[:].rearrange("p (r g) -> p r g", g=2), in_=bank[:].rearrange("p g r -> p r g"),
+                                 func=AF.Copy, bias=-1.0, scale=1.0)
+            nc.sync.dma_start(out=o1[:, a, CW * q:CW * (q + 1)], in_=res[:])
 
-        def store_mu(b):
-            lo, hi = banks[("mu", b)]
-            res = stage.tile([P, NA, 256], F32, name="mu", tag="mu")
-            nc.scalar.activation(out=res[:, 0:2, :], in_=lo[:], func=AF.Copy, bias=-1.0, scale=1.0)
-            nc.sync.dma_start(out=o1[:, 0:2, 256 * b:256 * (b + 1)], in_=res[:, 0:2, :])
-            nc.scalar.activation(out=res[:, 2, :], in_=hi[:], func=AF.Copy, bias=-1.0, scale=1.0)
-            nc.sync.dma_start(out=o1[:, 2, 256 * b:256 * (b + 1)], in_=res[:, 2, :])
+        def sum_region(q, a):
+            if a < 2:
+                return sums[(q, 0)][:, a, :]
+            return sums[(q, 1)][:]
 
-        def logs(b):
-            nc.scalar.activation(out=zt_[b][:], in_=st_[b][:], func=AF.Ln, scale=late_one[:, 0:1])
-            nc.scalar.activation(out=st_[b][:], in_=st_[b][:], func=AF.Ln, scale=-1.0, bias=late_one[:, 0:1])
-
-        def pair_sums(b, src, mat, first, last):
+        def add_sums(q, src, tiles, first, last):
             if first:
-                banks[("sc", b)] = psm.tile([P, NA, P], F32, name="sums", tag="sums")
-            sums = banks[("sc", b)]
-            for k, (a, c2) in enumerate(SPOTS):
-                nc.tensor.matmul(out=sums[:, a, c2 * 64:(c2 + 1) * 64], lhsT=src[:, c2, a * P:(a + 1) * P], rhs=mat[:],
-                                 start=(first and k == 0), stop=(last and k == len(SPOTS) - 1))
+                sums[(q, 0)] = psm.tile([P, 2, 256], F32, name="sumlo", tag="sums")
+                sums[(q, 1)] = psm.tile([P, 256], F32, name="sumhi", tag="sums")
+            for a in tiles:
+                region = sum_region(q, a)
+                opens = first and a in (0, 2)
+                closes = last and a in (1, 2)
+                spots = [(bl, h) for bl in range(2) for h in range(2)]
+                for k, (bl, h) in enumerate(spots):
+                    nc.tensor.matmul(out=region[:, bl * P:(bl + 1) * P], lhsT=src[:, bl, h, a * P:(a + 1) * P], rhs=ident[:],
+                                     is_transpose=True, start=(opens and k == 0), stop=(closes and k == len(spots) - 1))
 
-        def turn_var_scale(b):
-            banks[("var", b)] = turn_back(st_[b], None, b % 2 == 1)
-            pair_sums(b, zt_[b], shalf, False, True)
+        def log_unit(q, a):
+            view = st_[q][:, :, :, a * P:(a + 1) * P].rearrange("p b g t -> p (b g) t")
+            nc.scalar.activation(out=view, in_=view, func=AF.Ln, scale=-1.0, bias=late_one[:, 0:1])
 
-        def store_var_scale(b):
-            lo, hi = banks[("var", b)]
-            res = stage.tile([P, NA, 256], F32, name="var", tag="var")
-            nc.vector.scalar_tensor_tensor(out=res[:, 0:2, :].rearrange("p a c -> p (a c)"),
-                                           in0=lo[:].rearrange("p a c -> p (a c)"), scalar=0.5,
-                                           in1=v1x4[:, 0:2, :, :].rearrange("p a i c -> p (a i c)"),
+        def var_unit(q, a, k):
+            bank = turned_bank(k)
+            turn_unit(bank, st_[q], a, None)
+            res = stage.tile([P, CW], F32, name="var", tag="var")
+            nc.vector.scalar_tensor_tensor(out=res[:].rearrange("p (i c g) -> p i c g", i=8, g=2),
+                                           in0=bank[:].rearrange("p g (i c) -> p i c g", i=8), scalar=0.5,
+                                           in1=v1x[:, a, :].rearrange("p (c g) -> p c g", g=2).unsqueeze(1).to_broadcast([P, 8, 32, 2]),
                                            op0=ALU.mult, op1=ALU.add)
-            nc.sync.dma_start(out=o2[:, 0:2, 256 * b:256 * (b + 1)], in_=res[:, 0:2, :])
-            nc.vector.scalar_tensor_tensor(out=res[:, 2, :], in0=hi[:], scalar=0.5,
-                                           in1=v1x4[:, 2, :, :].rearrange("p i c -> p (i c)"),
+            nc.sync.dma_start(out=o2[:, a, CW * q:CW * (q + 1)], in_=res[:])
+
+        def scale_unit(q, a):
+            res0 = stage.tile([P, 256], F32, name="sc", tag="sc")
+            nc.vector.scalar_tensor_tensor(out=res0[:].rearrange("p (i c) -> p i c", i=8),
+                                           in0=sum_region(q, a).rearrange("p (i c) -> p i c", i=8), scalar=0.5,
+                                           in1=t0x[:, a, :].unsqueeze(1).to_broadcast([P, 8, 32]),
                                            op0=ALU.mult, op1=ALU.add)
-            nc.sync.dma_start(out=o2[:, 2, 256 * b:256 * (b + 1)], in_=res[:, 2, :])
-            sums = banks[("sc", b)]
-            res0 = stage.tile([P, NA, P], F32, name="sc", tag="sc")
-            nc.vector.tensor_tensor(out=res0[:].rearrange("p a (i c) -> p a i c", i=4),
-                                    in0=sums[:].rearrange("p a (i c) -> p a i c", i=4),
-                                    in1=t0x[:].unsqueeze(2).to_broadcast([P, NA, 4, 32]), op=ALU.add)
-            nc.sync.dma_start(out=o0[:, :, P * b:P * (b + 1)], in_=res0[:])
+            nc.sync.dma_start(out=o0[:, a, 256 * q:256 * (q + 1)], in_=res0[:])
 
-        def to_mu(b):
-            differences(b)
-            sigmoid(b)
-            product_w(b)
-            turn_mu(b)
-            store_mu(b)
+        def chunk_main(q):
+            for bl in range(2):
+                for h in range(2):
+                    project(q, bl, h)
+            for bl in range(2):
+                differences(q, bl)
+                sigmoid(q, bl)
+                product_w(q, bl)
+            for a in range(NA):
+                mu_unit(q, a)
+            add_sums(q, ut_[q], range(NA), True, False)
 
-        def prepare(q):
-            interleave("m", q)
-            interleave("v", q)
-            quantize_w("m", q)
-            quantize_w("v", q)
-
+        sv_flat = sv[:].rearrange("p a c -> p (a c)")
+        nc.scalar.activation(out=sg[:], in_=sv_flat, func=AF.Sigmoid, scale=-2.0)
+        nc.scalar.activation(out=sgc[:], in_=sv_flat, func=AF.Sigmoid, scale=2.0)
+        table_lay("v", sv[:], -2.0, 2.0)
+        table_lay("m", sm[:], 1.0, 1.0)
+        nie_lay()
         widen(0)
         interleave("m", 0)
         quantize_w("m", 0)
@@ -343,27 +340,33 @@ def tile_chainlveg_pa_kernel(tc, x, s_weight, s_mu, s_var, tcm_w, tcm_b,
         quantize_x()
         quantize_w("v", 0)
         bias_columns()
-        tables()
+        table_turn("v", tblv)
+        table_turn("m", m1p)
+        table_turn("n", nie1)
+        tables_small()
         widen(1)
-        for ct in range(4):
-            project(ct)
-        to_mu(0)
-        to_mu(1)
-        tables_late()
-        prepare(1)
-        for ct in range(4, 8):
-            project(ct)
-        to_mu(2)
-        to_mu(3)
-        nc.scalar.activation(out=late_one[:], in_=st_[NB - 1][:, 0, 0:1], func=AF.Copy, scale=0.0, bias=1.0)
-        for b0 in (0, 2):
-            product_q1(b0)
-            product_q1(b0 + 1)
-            product_q2(b0)
-            product_q2(b0 + 1)
-            pair_sums(b0, dt_[b0], shalf, True, False)
-            pair_sums(b0 + 1, dt_[b0 + 1], shalf, True, False)
-        for b in range(NB):
-            logs(b)
-            turn_var_scale(b)
-            store_var_scale(b)
+        chunk_main(0)
+        interleave("m", 1)
+        interleave("v", 1)
+        quantize_w("m", 1)
+        quantize_w("v", 1)
+        chunk_main(1)
+        nc.scalar.activation(out=late_one[:], in_=st_[NQ - 1][:, 1, 1, 0:1], func=AF.Copy, scale=0.0, bias=1.0)
+        for q in range(NQ):
+            product_q1(q, 0)
+            product_q1(q, 1)
+            product_q2(q, 0)
+            product_q2(q, 1)
+            add_sums(q, dt_[q], range(NA), False, False)
+        k = 0
+        for q in range(NQ):
+            for a in range(NA):
+                log_unit(q, a)
+                var_unit(q, a, k)
+                add_sums(q, st_[q], (a,), False, True)
+                if a == 1:
+                    scale_unit(q, 0)
+                    scale_unit(q, 1)
+                if a == 2:
+                    scale_unit(q, 2)
+                k += 1

@@ -26,6 +26,7 @@ LOG_2PI = math.log(2.0 * math.pi)
 FLOPS = 2 * TOK * KD * 2 * NCH
 
 TOKEN_WINDOWS = ((0, 256), (256, 128))
+VAR_ON_SCALAR = (2, 3, 4, 5)
 
 
 def tile_chainlveg_pa_kernel(tc, x, s_weight, s_mu, s_var, tcm_w, tcm_b,
@@ -234,7 +235,7 @@ def tile_chainlveg_pa_kernel(tc, x, s_weight, s_mu, s_var, tcm_w, tcm_b,
 
         def differences(q, bl):
             nc.vector.scalar_tensor_tensor(out=flat(ut_[q], bl), in0=flat(ut_[q], bl), scalar=4.0, in1=flat2(tblv),
-                                           op0=ALU.min, op1=ALU.subtract)
+                                           op0=ALU.min, op1=ALU.add)
             nc.vector.scalar_tensor_tensor(out=flat(dt_[q], bl), in0=flat(dt_[q], bl), scalar=2.0, in1=flat2(m1p),
                                            op0=ALU.min, op1=ALU.subtract)
 
@@ -298,8 +299,14 @@ def tile_chainlveg_pa_kernel(tc, x, s_weight, s_mu, s_var, tcm_w, tcm_b,
 
         def var_unit(q, a, k):
             bank = turned_bank(k)
-            turn_unit(bank, st_[q], a, None)
             res = stage.tile([P, CW], F32, name="var", tag="var")
+            if k in VAR_ON_SCALAR:
+                turn_unit(bank, st_[q], a, tblv)
+                nc.scalar.activation(out=res[:].rearrange("p (r g) -> p r g", g=2), in_=bank[:].rearrange("p g r -> p r g"),
+                                     func=AF.Copy, bias=1.0, scale=0.5)
+                nc.sync.dma_start(out=o2[:, a, CW * q:CW * (q + 1)], in_=res[:])
+                return
+            turn_unit(bank, st_[q], a, None)
             nc.vector.scalar_tensor_tensor(out=res[:].rearrange("p (i c g) -> p i c g", i=8, g=2),
                                            in0=bank[:].rearrange("p g (i c) -> p i c g", i=8), scalar=0.5,
                                            in1=v1x[:, a, :].rearrange("p (c g) -> p c g", g=2).unsqueeze(1).to_broadcast([P, 8, 32, 2]),
@@ -329,7 +336,7 @@ def tile_chainlveg_pa_kernel(tc, x, s_weight, s_mu, s_var, tcm_w, tcm_b,
         sv_flat = sv[:].rearrange("p a c -> p (a c)")
         nc.scalar.activation(out=sg[:], in_=sv_flat, func=AF.Sigmoid, scale=-2.0)
         nc.scalar.activation(out=sgc[:], in_=sv_flat, func=AF.Sigmoid, scale=2.0)
-        table_lay("v", sv[:], -2.0, 2.0)
+        table_lay("v", sv[:], 2.0, -2.0)
         table_lay("m", sm[:], 1.0, 1.0)
         nie_lay()
         widen(0)

@@ -26,7 +26,7 @@ LOG_2PI = math.log(2.0 * math.pi)
 FLOPS = 2 * TOK * KD * 2 * NCH
 
 TOKEN_WINDOWS = ((0, 256), (256, 128))
-VAR_ON_SCALAR = (2, 3, 4, 5)
+VAR_ON_SCALAR = ()
 
 
 def tile_chainlveg_pa_kernel(tc, x, s_weight, s_mu, s_var, tcm_w, tcm_b,
@@ -82,11 +82,6 @@ def tile_chainlveg_pa_kernel(tc, x, s_weight, s_mu, s_var, tcm_w, tcm_b,
         load_v(1)
         for a in range(NA):
             nc.sync.dma_start(out=xs[:, a, :], in_=xv[:, a, :])
-        nc.sync.dma_start(out=brow[0:4, :], in_=tcm_b.rearrange("(c q) -> c q", q=256))
-        nc.sync.dma_start(out=brow[4:8, :], in_=tcv_b.rearrange("(c q) -> c q", q=256))
-        nc.sync.dma_start(out=sw[:], in_=swv)
-        load_m(1, 0)
-        load_m(1, 1)
 
         ident = keep.tile([P, P], F32, name="ident")
         make_identity(nc, ident[:])
@@ -113,24 +108,42 @@ def tile_chainlveg_pa_kernel(tc, x, s_weight, s_mu, s_var, tcm_w, tcm_b,
             nc.vector.tensor_scalar(out=biasm[:], in0=bt[:, :, 0:4], scalar1=1.0, scalar2=None, op0=ALU.add)
             nc.vector.tensor_scalar(out=biasv[:], in0=bt[:, :, 4:8], scalar1=-2.0, scalar2=2.0, op0=ALU.mult, op1=ALU.add)
 
-        bigs = {}
+        scratch = out_0.rearrange("b p i j t e -> (b p i j t e)").rearrange("(s r c) -> s r c", s=4, r=P)
+        comp = {}
+        for k in range(2):
+            comp[k] = keep.tile([P, NA, P], F32, name="comp%d" % k)
+        nc.gpsimd.memset(comp[1][:, :, 64:P], 0.0)
+        aff = keep.tile([P, 2], F32, name="aff")
+        nc.vector.memset(aff[0:64, 0:1], 2.0)
+        nc.vector.memset(aff[0:64, 1:2], -2.0)
+        nc.vector.memset(aff[64:P, :], 1.0)
 
-        def table_lay(label, src3, mul, add):
-            y = keep.tile([P, NA, 2, 32], F32, name="y" + label)
-            nc.vector.tensor_copy(out=y[:].rearrange("p a g (j t) -> p a g j t", t=2),
+        def compact_lay(k, half, src3):
+            nc.vector.tensor_copy(out=comp[k][:, :, 64 * half:64 * (half + 1)].rearrange("p a (g j t) -> p a g j t", g=2, t=2),
                                   in_=src3.rearrange("p a (j g) -> p a g j", g=2).unsqueeze(4).to_broadcast([P, NA, 2, 16, 2]))
-            big = keep.tile([P, NA * 2, 4, 32], F32, name="big" + label)
-            nc.vector.tensor_scalar(out=big[:], in0=y[:].rearrange("p a g c -> p (a g) c").unsqueeze(2).to_broadcast([P, NA * 2, 4, 32]),
-                                    scalar1=mul, scalar2=add, op0=ALU.mult, op1=ALU.add)
-            bigs[label] = big
 
-        def table_turn(label, dst):
-            big = bigs[label]
-            for g in range(2):
-                tq = psm.tile([P, TOK], F32, name="tq", tag="sums")
-                for a in range(NA):
-                    nc.tensor.transpose(tq[:, a * P:(a + 1) * P], big[:, a * 2 + g, :, :].rearrange("p i c -> p (i c)"), ident[:])
-                nc.scalar.copy(out=dst[:, g, :], in_=tq[:])
+        def compact_turn(k):
+            tq = psm.tile([P, TOK], F32, name="tq", tag="sums")
+            for a in range(NA):
+                nc.tensor.transpose(tq[:, a * P:(a + 1) * P], comp[k][:, a, :], ident[:])
+            ct = keep.tile([P, TOK], F32, name="ct%d" % k)
+            if k == 0:
+                nc.scalar.activation(out=ct[:], in_=tq[:], func=AF.Identity, scale=aff[:, 0:1], bias=aff[:, 1:2])
+            else:
+                nc.scalar.copy(out=ct[:], in_=tq[:])
+            nc.sync.dma_start(out=scratch[k], in_=ct[:])
+
+        def table_back(k, half, dst):
+            for i4 in range(4):
+                nc.sync.dma_start(out=dst[32 * i4:32 * (i4 + 1), :, :],
+                                  in_=scratch[k, 64 * half:64 * (half + 1), :].rearrange("(g r) c -> r g c", g=2))
+
+        def nie_lay():
+            rc = keep.tile([P, 96], F32, name="rc")
+            nc.vector.reciprocal(out=rc[:], in_=sgc[:])
+            nie = keep.tile([P, 96], F32, name="nie")
+            nc.vector.scalar_tensor_tensor(out=nie[:], in0=sg[:], scalar=-1.0, in1=rc[:], op0=ALU.mult, op1=ALU.mult)
+            compact_lay(1, 0, nie[:].rearrange("p (a c) -> p a c", a=NA))
 
         def tables_small():
             nc.vector.tensor_copy(
@@ -145,13 +158,6 @@ def tile_chainlveg_pa_kernel(tc, x, s_weight, s_mu, s_var, tcm_w, tcm_b,
                 scalar=-LOG_2PI,
                 in1=vsum[:].unsqueeze(2).to_broadcast([P, 48, 2]),
                 op0=ALU.add, op1=ALU.subtract)
-
-        def nie_lay():
-            rc = keep.tile([P, 96], F32, name="rc")
-            nc.vector.reciprocal(out=rc[:], in_=sgc[:])
-            nie = keep.tile([P, 96], F32, name="nie")
-            nc.vector.scalar_tensor_tensor(out=nie[:], in0=sg[:], scalar=-1.0, in1=rc[:], op0=ALU.mult, op1=ALU.mult)
-            table_lay("n", nie[:].rearrange("p (a c) -> p a c", a=NA), 1.0, 0.0)
 
         wcod = {}
         wscl = {}
@@ -336,9 +342,19 @@ def tile_chainlveg_pa_kernel(tc, x, s_weight, s_mu, s_var, tcm_w, tcm_b,
         sv_flat = sv[:].rearrange("p a c -> p (a c)")
         nc.scalar.activation(out=sg[:], in_=sv_flat, func=AF.Sigmoid, scale=-2.0)
         nc.scalar.activation(out=sgc[:], in_=sv_flat, func=AF.Sigmoid, scale=2.0)
-        table_lay("v", sv[:], 2.0, -2.0)
-        table_lay("m", sm[:], 1.0, 1.0)
+        compact_lay(0, 0, sv[:])
+        compact_lay(0, 1, sm[:])
+        compact_turn(0)
+        table_back(0, 0, tblv)
+        table_back(0, 1, m1p)
+        nc.sync.dma_start(out=brow[0:4, :], in_=tcm_b.rearrange("(c q) -> c q", q=256))
+        nc.sync.dma_start(out=brow[4:8, :], in_=tcv_b.rearrange("(c q) -> c q", q=256))
+        nc.sync.dma_start(out=sw[:], in_=swv)
+        load_m(1, 0)
+        load_m(1, 1)
         nie_lay()
+        compact_turn(1)
+        table_back(1, 0, nie1)
         widen(0)
         interleave("m", 0)
         quantize_w("m", 0)
@@ -347,9 +363,6 @@ def tile_chainlveg_pa_kernel(tc, x, s_weight, s_mu, s_var, tcm_w, tcm_b,
         quantize_x()
         quantize_w("v", 0)
         bias_columns()
-        table_turn("v", tblv)
-        table_turn("m", m1p)
-        table_turn("n", nie1)
         tables_small()
         widen(1)
         chunk_main(0)

@@ -27,6 +27,7 @@ FLOPS = 2 * TOK * KD * 2 * NCH
 
 TOKEN_WINDOWS = ((0, 256), (256, 128))
 VAR_ON_SCALAR = ()
+WIDEN_ON_VECTOR = ((1, 1),)
 
 
 def tile_chainlveg_pa_kernel(tc, x, s_weight, s_mu, s_var, tcm_w, tcm_b,
@@ -171,8 +172,12 @@ def tile_chainlveg_pa_kernel(tc, x, s_weight, s_mu, s_var, tcm_w, tcm_b,
             for g in range(NG):
                 t = keep.tile([P, 4, CW], BF16, name="wide%d%d" % (g, q))
                 for j in range(4):
-                    nc.scalar.activation(out=t[:, j, :], in_=vbytes[g][:, j, CW * q:CW * (q + 1)].bitcast(FP8),
-                                         func=AF.Copy, scale=vsc[:, g, j:j + 1])
+                    if (g, q) in WIDEN_ON_VECTOR:
+                        nc.vector.tensor_scalar(out=t[:, j, :], in0=vbytes[g][:, j, CW * q:CW * (q + 1)].bitcast(FP8),
+                                                scalar1=vsc[:, g, j:j + 1], scalar2=None, op0=ALU.mult)
+                    else:
+                        nc.scalar.activation(out=t[:, j, :], in_=vbytes[g][:, j, CW * q:CW * (q + 1)].bitcast(FP8),
+                                             func=AF.Copy, scale=vsc[:, g, j:j + 1])
                 wide[(g, q)] = t
 
         def interleave(nm, q):

@@ -263,9 +263,9 @@ def tile_chainlveg_pa_kernel(tc, x, s_weight, s_mu, s_var, tcm_w, tcm_b,
             nc.vector.tensor_tensor(out=flat(dt_[q], bl), in0=flat(dt_[q], bl), in1=flat2(nie1), op=ALU.mult)
 
         def turned_bank(k):
-            if k % 2 == 0:
+            if k % 4 < 2:
                 return ptr.tile([P, 2, 256], F32, name="tb", tag="tr")
-            return pmx.tile([P, 2, 256], F32, name="tb2", tag=("pm" if k % 4 == 1 else "pv"))
+            return pmx.tile([P, 2, 256], F32, name="tb2", tag=("pm" if k % 4 == 2 else "pv"))
 
         def turn_unit(bank, src, a, table):
             spots = [(h, bl) for h in range(2) for bl in range(2)]
@@ -279,7 +279,7 @@ def tile_chainlveg_pa_kernel(tc, x, s_weight, s_mu, s_var, tcm_w, tcm_b,
                                  start=(table is None and k == 0), stop=(k == len(spots) - 1))
 
         def mu_unit(q, a):
-            bank = ptr.tile([P, 2, 256], F32, name="tb", tag="tr")
+            bank = turned_bank(a) if q == NQ - 1 else ptr.tile([P, 2, 256], F32, name="tb", tag="tr")
             turn_unit(bank, wt_[q], a, m1p)
             res = stage.tile([P, CW], F32, name="mu", tag="mu")
             nc.scalar.activation(out=res[:].rearrange("p (r g) -> p r g", g=2), in_=bank[:].rearrange("p g r -> p r g"),
@@ -309,7 +309,7 @@ def tile_chainlveg_pa_kernel(tc, x, s_weight, s_mu, s_var, tcm_w, tcm_b,
             nc.scalar.activation(out=view, in_=view, func=AF.Ln, scale=-1.0, bias=late_one[:, 0:1])
 
         def var_unit(q, a, k):
-            bank = turned_bank(k)
+            bank = turned_bank(k + NA)
             res = stage.tile([P, CW], F32, name="var", tag="var")
             if k in VAR_ON_SCALAR:
                 turn_unit(bank, st_[q], a, tblv)

@@ -47,7 +47,7 @@ def tile_chainlveg_pa_kernel(tc, x, s_weight, s_mu, s_var, tcm_w, tcm_b,
         stage = ctx.enter_context(tc.tile_pool(name="stage", bufs=3))
         pmx = ctx.enter_context(tc.psum_pool(name="pmx", bufs=1))
         ptr = ctx.enter_context(tc.psum_pool(name="ptr", bufs=2))
-        psm = ctx.enter_context(tc.psum_pool(name="psm", bufs=4))
+        psm = ctx.enter_context(tc.psum_pool(name="psm", bufs=1))
 
         sv = keep.tile([P, NA, 32], BF16, name="sv")
         sm = keep.tile([P, NA, 32], BF16, name="sm")
@@ -124,7 +124,7 @@ def tile_chainlveg_pa_kernel(tc, x, s_weight, s_mu, s_var, tcm_w, tcm_b,
                                   in_=src3.rearrange("p a (j g) -> p a g j", g=2).unsqueeze(4).to_broadcast([P, NA, 2, 16, 2]))
 
         def compact_turn(k):
-            tq = psm.tile([P, TOK], F32, name="tq", tag="sums")
+            tq = psm.tile([P, TOK], F32, name="tq", tag="s%d" % (2 + k))
             for a in range(NA):
                 nc.tensor.transpose(tq[:, a * P:(a + 1) * P], comp[k][:, a, :], ident[:])
             ct = keep.tile([P, TOK], F32, name="ct%d" % k)
@@ -229,7 +229,10 @@ def tile_chainlveg_pa_kernel(tc, x, s_weight, s_mu, s_var, tcm_w, tcm_b,
             cols = slice(c0, c0 + P)
             blk = 2 * q + bl
             for nm, tg, dst, bias, mul in (("v", "pv", ut_[q], biasv, -2.0), ("m", "pm", dt_[q], biasm, 1.0)):
-                acc = pmx.tile([P, TOK], F32, name="acc" + nm, tag=tg)
+                if h == 0:
+                    acc = pmx.tile([P, TOK], F32, name="acc" + nm, tag=tg)
+                else:
+                    acc = psm.tile([P, TOK], F32, name="acc" + nm, tag=("s2" if nm == "v" else "s3"))
                 for t0, tw in TOKEN_WINDOWS:
                     for g in range(NG):
                         nc.tensor.matmul_mx(out=acc[:, t0:t0 + tw],
@@ -293,8 +296,8 @@ def tile_chainlveg_pa_kernel(tc, x, s_weight, s_mu, s_var, tcm_w, tcm_b,
 
         def add_sums(q, src, tiles, first, last):
             if first:
-                sums[(q, 0)] = psm.tile([P, 2, 256], F32, name="sumlo", tag="sums")
-                sums[(q, 1)] = psm.tile([P, 256], F32, name="sumhi", tag="sums")
+                sums[(q, 0)] = psm.tile([P, 2, 256], F32, name="sumlo", tag="s%d" % (2 * q))
+                sums[(q, 1)] = psm.tile([P, 256], F32, name="sumhi", tag="s%d" % (2 * q + 1))
             for a in tiles:
                 region = sum_region(q, a)
                 opens = first and a in (0, 2)

@@ -217,29 +217,38 @@ def tile_chainlveg_pa_kernel(tc, x, s_weight, s_mu, s_var, tcm_w, tcm_b,
         dt_ = {}
         st_ = {}
         wt_ = {}
+        lt_ = {}
         for q in range(NQ):
             ut_[q] = keep.tile([P, 2, 2, TOK], F32, name="uu%d" % q)
             dt_[q] = keep.tile([P, 2, 2, TOK], F32, name="dd%d" % q)
             st_[q] = keep.tile([P, 2, 2, TOK], F32, name="ss%d" % q)
             wt_[q] = keep.tile([P, 2, 2, TOK], F32, name="ww%d" % q)
+            lt_[q] = keep.tile([P, 2, 2, TOK], F32, name="ll%d" % q)
         sums = {}
 
-        def project(q, bl, h):
+        def project_one(nm, q, bl, h, where):
             c0 = CW * q + 256 * h + P * bl
             cols = slice(c0, c0 + P)
             blk = 2 * q + bl
-            for nm, tg, dst, bias, mul in (("v", "pv", ut_[q], biasv, -2.0), ("m", "pm", dt_[q], biasm, 1.0)):
-                if h == 0:
-                    acc = pmx.tile([P, TOK], F32, name="acc" + nm, tag=tg)
-                else:
-                    acc = psm.tile([P, TOK], F32, name="acc" + nm, tag=("s2" if nm == "v" else "s3"))
-                for t0, tw in TOKEN_WINDOWS:
-                    for g in range(NG):
-                        nc.tensor.matmul_mx(out=acc[:, t0:t0 + tw],
-                                            lhsT=wcod[nm][:, g, cols].bitcast(FP8X4), lhsT_scale=wscl[nm][:, g, cols],
-                                            rhs=xcod[:, g, t0:t0 + tw].bitcast(FP8X4), rhs_scale=xscl[:, g, t0:t0 + tw],
-                                            start=(g == 0), stop=(g == NG - 1))
-                nc.scalar.activation(out=dst[:, bl, h, :], in_=acc[:], func=AF.Relu, bias=bias[:, h, blk:blk + 1], scale=mul)
+            dst, bias, mul = (ut_[q], biasv, -2.0) if nm == "v" else (dt_[q], biasm, 1.0)
+            acc = where[0].tile([P, TOK], F32, name="acc" + nm, tag=where[1])
+            for t0, tw in TOKEN_WINDOWS:
+                for g in range(NG):
+                    nc.tensor.matmul_mx(out=acc[:, t0:t0 + tw],
+                                        lhsT=wcod[nm][:, g, cols].bitcast(FP8X4), lhsT_scale=wscl[nm][:, g, cols],
+                                        rhs=xcod[:, g, t0:t0 + tw].bitcast(FP8X4), rhs_scale=xscl[:, g, t0:t0 + tw],
+                                        start=(g == 0), stop=(g == NG - 1))
+            nc.scalar.activation(out=dst[:, bl, h, :], in_=acc[:], func=AF.Relu, bias=bias[:, h, blk:blk + 1], scale=mul)
+
+        def project(q, bl, h):
+            project_one("v", q, bl, h, (pmx, "pv") if h == 0 else (psm, "s2"))
+            project_one("m", q, bl, h, (pmx, "pm") if h == 0 else (psm, "s3"))
+
+        def project_matrix(nm, q):
+            banks = ((pmx, "pv"), (psm, "s2"), (pmx, "pm"), (psm, "s3"))
+            for bl in range(2):
+                for h in range(2):
+                    project_one(nm, q, bl, h, banks[2 * bl + h])
 
         def flat(t, bl):
             return t[:, bl, :, :].rearrange("p g t -> p (g t)")
@@ -247,9 +256,11 @@ def tile_chainlveg_pa_kernel(tc, x, s_weight, s_mu, s_var, tcm_w, tcm_b,
         def flat2(t):
             return t[:].rearrange("p g t -> p (g t)")
 
-        def differences(q, bl):
+        def difference_u(q, bl):
             nc.vector.scalar_tensor_tensor(out=flat(ut_[q], bl), in0=flat(ut_[q], bl), scalar=4.0, in1=flat2(tblv),
                                            op0=ALU.min, op1=ALU.add)
+
+        def difference_d(q, bl):
             nc.vector.scalar_tensor_tensor(out=flat(dt_[q], bl), in0=flat(dt_[q], bl), scalar=2.0, in1=flat2(m1p),
                                            op0=ALU.min, op1=ALU.subtract)
 
@@ -261,6 +272,16 @@ def tile_chainlveg_pa_kernel(tc, x, s_weight, s_mu, s_var, tcm_w, tcm_b,
 
         def product_q1(q, bl):
             nc.vector.tensor_tensor(out=flat(dt_[q], bl), in0=flat(wt_[q], bl), in1=flat(dt_[q], bl), op=ALU.mult)
+
+        def slab(t, a):
+            return t[:, :, :, a * P:(a + 1) * P].rearrange("p b g t -> p (b g) t")
+
+        def product_q1_tile(q, a):
+            nc.vector.tensor_tensor(out=slab(dt_[q], a), in0=slab(wt_[q], a), in1=slab(dt_[q], a), op=ALU.mult)
+
+        def product_q2_tile(q, a):
+            nc.vector.tensor_tensor(out=dt_[q][:, :, :, a * P:(a + 1) * P], in0=dt_[q][:, :, :, a * P:(a + 1) * P],
+                                    in1=nie1[:, :, a * P:(a + 1) * P].unsqueeze(1).to_broadcast([P, 2, 2, P]), op=ALU.mult)
 
         def product_q2(q, bl):
             nc.vector.tensor_tensor(out=flat(dt_[q], bl), in0=flat(dt_[q], bl), in1=flat2(nie1), op=ALU.mult)
@@ -308,19 +329,20 @@ def tile_chainlveg_pa_kernel(tc, x, s_weight, s_mu, s_var, tcm_w, tcm_b,
                                      is_transpose=True, start=(opens and k == 0), stop=(closes and k == len(spots) - 1))
 
         def log_unit(q, a):
-            view = st_[q][:, :, :, a * P:(a + 1) * P].rearrange("p b g t -> p (b g) t")
-            nc.scalar.activation(out=view, in_=view, func=AF.Ln, scale=-1.0, bias=late_one[:, 0:1])
+            nc.scalar.activation(out=lt_[q][:, :, :, a * P:(a + 1) * P].rearrange("p b g t -> p (b g) t"),
+                                 in_=st_[q][:, :, :, a * P:(a + 1) * P].rearrange("p b g t -> p (b g) t"),
+                                 func=AF.Ln, scale=-1.0, bias=late_one[:, 0:1])
 
         def var_unit(q, a, k):
-            bank = turned_bank(k + NA)
+            bank = turned_bank(k) if q == NQ - 1 else ptr.tile([P, 2, 256], F32, name="tb", tag="tr")
             res = stage.tile([P, CW], F32, name="var", tag="var")
             if k in VAR_ON_SCALAR:
-                turn_unit(bank, st_[q], a, tblv)
+                turn_unit(bank, lt_[q], a, tblv)
                 nc.scalar.activation(out=res[:].rearrange("p (r g) -> p r g", g=2), in_=bank[:].rearrange("p g r -> p r g"),
                                      func=AF.Copy, bias=1.0, scale=0.5)
                 nc.sync.dma_start(out=o2[:, a, CW * q:CW * (q + 1)], in_=res[:])
                 return
-            turn_unit(bank, st_[q], a, None)
+            turn_unit(bank, lt_[q], a, None)
             nc.vector.scalar_tensor_tensor(out=res[:].rearrange("p (i c g) -> p i c g", i=8, g=2),
                                            in0=bank[:].rearrange("p g (i c) -> p i c g", i=8), scalar=0.5,
                                            in1=v1x[:, a, :].rearrange("p (c g) -> p c g", g=2).unsqueeze(1).to_broadcast([P, 8, 32, 2]),
@@ -340,7 +362,8 @@ def tile_chainlveg_pa_kernel(tc, x, s_weight, s_mu, s_var, tcm_w, tcm_b,
                 for h in range(2):
                     project(q, bl, h)
             for bl in range(2):
-                differences(q, bl)
+                difference_u(q, bl)
+                difference_d(q, bl)
                 sigmoid(q, bl)
                 product_w(q, bl)
             for a in range(NA):
@@ -374,27 +397,43 @@ def tile_chainlveg_pa_kernel(tc, x, s_weight, s_mu, s_var, tcm_w, tcm_b,
         tables_small()
         widen(1)
         chunk_main(0)
-        interleave("m", 1)
         interleave("v", 1)
-        quantize_w("m", 1)
         quantize_w("v", 1)
-        chunk_main(1)
+        project_matrix("v", 1)
+        for bl in range(2):
+            difference_u(1, bl)
+            sigmoid(1, bl)
         nc.scalar.activation(out=late_one[:], in_=st_[NQ - 1][:, 1, 1, 0:1], func=AF.Copy, scale=0.0, bias=1.0)
+        interleave("m", 1)
+        quantize_w("m", 1)
+        project_matrix("m", 1)
+        for bl in range(2):
+            difference_d(1, bl)
+            product_w(1, bl)
         for q in range(NQ):
-            product_q1(q, 0)
-            product_q1(q, 1)
-            product_q2(q, 0)
-            product_q2(q, 1)
-            add_sums(q, dt_[q], range(NA), False, False)
-        k = 0
-        for q in range(NQ):
+            if q == 1:
+                for a in range(NA):
+                    mu_unit(1, a)
+                add_sums(1, ut_[1], range(NA), True, False)
             for a in range(NA):
                 log_unit(q, a)
-                var_unit(q, a, k)
-                add_sums(q, st_[q], (a,), False, True)
-                if a == 1:
-                    scale_unit(q, 0)
-                    scale_unit(q, 1)
-                if a == 2:
-                    scale_unit(q, 2)
-                k += 1
+                var_unit(q, a, NA * q + a)
+            add_sums(q, lt_[q], range(NA), False, False)
+            if q == 0:
+                product_q1(q, 0)
+                product_q1(q, 1)
+                product_q2(q, 0)
+                product_q2(q, 1)
+                add_sums(q, dt_[q], range(NA), False, True)
+                for a in range(NA):
+                    scale_unit(q, a)
+            else:
+                for a in (2, 0, 1):
+                    product_q1_tile(q, a)
+                for a in (2, 0, 1):
+                    product_q2_tile(q, a)
+                    add_sums(q, dt_[q], (a,), False, True)
+                    if a == 2:
+                        scale_unit(q, 2)
+                scale_unit(q, 0)
+                scale_unit(q, 1)

from contextlib import ExitStack
import math

import concourse.mybir as mybir
from concourse.masks import make_identity

F32 = mybir.dt.float32
BF16 = mybir.dt.bfloat16
U8 = mybir.dt.uint8
U32 = mybir.dt.uint32
FP8 = mybir.dt.float8_e4m3fn
FP8X4 = mybir.dt.float8_e4m3fn_x4
AF = mybir.ActivationFunctionType
ALU = mybir.AluOpType

P = 128
TOK = 384
NA = 3
KD = 1024
NG = 2
NCH = 1024
NQ = 2
CW = 512
LOG_2PI = math.log(2.0 * math.pi)

FLOPS = 2 * TOK * KD * 2 * NCH

TOKEN_WINDOWS = ((0, 256), (256, 128))
VAR_ON_SCALAR = ()
WIDEN_ON_VECTOR = ((1, 1),)


def tile_chainlveg_pa_kernel(tc, x, s_weight, s_mu, s_var, tcm_w, tcm_b,
                                         tcv_w_bytes, tcv_w_scale, tcv_b, out_0, out_1, out_2):
    nc = tc.nc

    xv = x.rearrange("b p d -> (b p) d").rearrange("(a q) d -> q a d", q=P)
    smv = s_mu.rearrange("b p j e g -> (b p) (j e g)").rearrange("(a q) c -> q a c", q=P)
    svv = s_var.rearrange("b p j e g -> (b p) (j e g)").rearrange("(a q) c -> q a c", q=P)
    swv = s_weight.rearrange("b p j e -> (b p) (j e)").rearrange("(a q) c -> q a c", q=P)
    o0 = out_0.rearrange("b p i j t e -> (b p) (i j t e)").rearrange("(a q) c -> q a c", q=P)
    o1 = out_1.rearrange("b p i j t e g -> (b p) (i j t e g)").rearrange("(a q) c -> q a c", q=P)
    o2 = out_2.rearrange("b p i j t e g -> (b p) (i j t e g)").rearrange("(a q) c -> q a c", q=P)

    with ExitStack() as ctx:
        keep = ctx.enter_context(tc.tile_pool(name="keep", bufs=1))
        stage = ctx.enter_context(tc.tile_pool(name="stage", bufs=3))
        pmx = ctx.enter_context(tc.psum_pool(name="pmx", bufs=1))
        ptr = ctx.enter_context(tc.psum_pool(name="ptr", bufs=2))
        psm = ctx.enter_context(tc.psum_pool(name="psm", bufs=1))

        sv = keep.tile([P, NA, 32], BF16, name="sv")
        sm = keep.tile([P, NA, 32], BF16, name="sm")
        sw = keep.tile([P, NA, 16], BF16, name="sw")
        vsc = keep.tile([P, NG, 4], F32, name="vsc")
        brow = keep.tile([P, 256], BF16, name="brow")
        nc.vector.memset(brow[:], 0.0)
        warm = keep.tile([P, 1], F32, name="warm")
        nc.vector.memset(warm[:], 0.0)
        warm2 = keep.tile([P, 1], F32, name="warm2")
        nc.scalar.activation(out=warm2[:], in_=warm[:], func=AF.Sigmoid)

        vbytes = {}
        rawm = {}
        xs = keep.tile([P, NA, KD], BF16, name="xs")

        def load_v(g):
            t = keep.tile([P, 4, NCH], U8, name="vbytes%d" % g)
            vbytes[g] = t
            nc.sync.dma_start(out=t[:], in_=tcv_w_bytes[512 * g:512 * (g + 1), :].rearrange("(p j) n -> p j n", j=4))

        def load_m(q, g):
            t = keep.tile([P, 4, CW], BF16, name="rawm%d%d" % (g, q))
            rawm[(g, q)] = t
            nc.sync.dma_start(out=t[:], in_=tcm_w[512 * g:512 * (g + 1), CW * q:CW * (q + 1)].rearrange("(p j) n -> p j n", j=4))

        nc.sync.dma_start(out=vsc[:], in_=tcv_w_scale.rearrange("(g p t) o -> p g (t o)", p=P, t=4))
        nc.sync.dma_start(out=sv[:], in_=svv)
        nc.sync.dma_start(out=sm[:], in_=smv)
        load_m(0, 0)
        load_v(0)
        load_m(0, 1)
        load_v(1)
        for a in range(NA):
            nc.sync.dma_start(out=xs[:, a, :], in_=xv[:, a, :])

        ident = keep.tile([P, P], F32, name="ident")
        make_identity(nc, ident[:])
        identb = keep.tile([P, P], BF16, name="identb")
        make_identity(nc, identb[:])
        late_one = keep.tile([P, 1], F32, name="late_one")

        v1x = keep.tile([P, NA, 64], F32, name="v1x")
        t0x = keep.tile([P, NA, 32], F32, name="t0x")
        biasm = keep.tile([P, 2, 4], F32, name="biasm")
        biasv = keep.tile([P, 2, 4], F32, name="biasv")
        tblv = keep.tile([P, 2, TOK], F32, name="tblv")
        m1p = keep.tile([P, 2, TOK], F32, name="m1p")
        nie1 = keep.tile([P, 2, TOK], F32, name="nie1")
        sg = keep.tile([P, 96], F32, name="sg")
        sgc = keep.tile([P, 96], F32, name="sgc")

        def bias_columns():
            browg = keep.tile([P, 2, P], BF16, name="browg")
            nc.vector.tensor_copy(out=browg[:], in_=brow[:].rearrange("p (m g) -> p g m", g=2))
            bt = ptr.tile([P, 2, P], BF16, name="bt", tag="tr")
            for g in range(2):
                nc.tensor.transpose(bt[:, g, :], browg[:, g, :], identb[:])
            nc.vector.tensor_scalar(out=biasm[:], in0=bt[:, :, 0:4], scalar1=1.0, scalar2=None, op0=ALU.add)
            nc.vector.tensor_scalar(out=biasv[:], in0=bt[:, :, 4:8], scalar1=-2.0, scalar2=2.0, op0=ALU.mult, op1=ALU.add)

        scratch = out_0.rearrange("b p i j t e -> (b p i j t e)").rearrange("(s r c) -> s r c", s=4, r=P)
        comp = {}
        for k in range(2):
            comp[k] = keep.tile([P, NA, P], F32, name="comp%d" % k)
        nc.gpsimd.memset(comp[1][:, :, 64:P], 0.0)
        aff = keep.tile([P, 2], F32, name="aff")
        nc.vector.memset(aff[0:64, 0:1], 2.0)
        nc.vector.memset(aff[0:64, 1:2], -2.0)
        nc.vector.memset(aff[64:P, :], 1.0)

        def compact_lay(k, half, src3):
            nc.vector.tensor_copy(out=comp[k][:, :, 64 * half:64 * (half + 1)].rearrange("p a (g j t) -> p a g j t", g=2, t=2),
                                  in_=src3.rearrange("p a (j g) -> p a g j", g=2).unsqueeze(4).to_broadcast([P, NA, 2, 16, 2]))

        def compact_turn(k):
            tq = psm.tile([P, TOK], F32, name="tq", tag="s%d" % (2 + k))
            for a in range(NA):
                nc.tensor.transpose(tq[:, a * P:(a + 1) * P], comp[k][:, a, :], ident[:])
            ct = keep.tile([P, TOK], F32, name="ct%d" % k)
            if k == 0:
                nc.scalar.activation(out=ct[:], in_=tq[:], func=AF.Identity, scale=aff[:, 0:1], bias=aff[:, 1:2])
            else:
                nc.scalar.copy(out=ct[:], in_=tq[:])
            nc.sync.dma_start(out=scratch[k], in_=ct[:])

        def table_back(k, half, dst):
            for i4 in range(4):
                nc.sync.dma_start(out=dst[32 * i4:32 * (i4 + 1), :, :],
                                  in_=scratch[k, 64 * half:64 * (half + 1), :].rearrange("(g r) c -> r g c", g=2))

        def nie_lay():
            rc = keep.tile([P, 96], F32, name="rc")
            nc.vector.reciprocal(out=rc[:], in_=sgc[:])
            nie = keep.tile([P, 96], F32, name="nie")
            nc.vector.scalar_tensor_tensor(out=nie[:], in0=sg[:], scalar=-1.0, in1=rc[:], op0=ALU.mult, op1=ALU.mult)
            compact_lay(1, 0, nie[:].rearrange("p (a c) -> p a c", a=NA))

        def tables_small():
            nc.vector.tensor_copy(
                out=v1x[:].rearrange("p a (j t g) -> p (a j) t g", t=2, g=2),
                in_=sv[:].rearrange("p a (j g) -> p (a j) g", g=2).unsqueeze(2).to_broadcast([P, 48, 2, 2]))
            svp = sv[:].rearrange("p a (j g) -> p (a j) g", g=2)
            vsum = keep.tile([P, 48], F32, name="vsum")
            nc.vector.tensor_tensor(out=vsum[:], in0=svp[:, :, 0], in1=svp[:, :, 1], op=ALU.add)
            nc.vector.scalar_tensor_tensor(
                out=t0x[:].rearrange("p a (j t) -> p (a j) t", t=2),
                in0=sw[:].rearrange("p a j -> p (a j)").unsqueeze(2).to_broadcast([P, 48, 2]),
                scalar=-LOG_2PI,
                in1=vsum[:].unsqueeze(2).to_broadcast([P, 48, 2]),
                op0=ALU.add, op1=ALU.subtract)

        wcod = {}
        wscl = {}
        for nm in ("m", "v"):
            wcod[nm] = keep.tile([P, NG, NCH], U32, name="wcod" + nm, align_bytes=64)
            wscl[nm] = keep.tile([P, NG, NCH], U8, name="wscl" + nm, align_bytes=64)
        wide = {}
        grouped = {}

        def widen(q):
            for g in range(NG):
                t = keep.tile([P, 4, CW], BF16, name="wide%d%d" % (g, q))
                for j in range(4):
                    if (g, q) in WIDEN_ON_VECTOR:
                        nc.vector.tensor_scalar(out=t[:, j, :], in0=vbytes[g][:, j, CW * q:CW * (q + 1)].bitcast(FP8),
                                                scalar1=vsc[:, g, j:j + 1], scalar2=None, op0=ALU.mult)
                    else:
                        nc.scalar.activation(out=t[:, j, :], in_=vbytes[g][:, j, CW * q:CW * (q + 1)].bitcast(FP8),
                                             func=AF.Copy, scale=vsc[:, g, j:j + 1])
                wide[(g, q)] = t

        def interleave(nm, q):
            for g in range(NG):
                src = rawm[(g, q)] if nm == "m" else wide[(g, q)]
                t = keep.tile([P, CW, 4], BF16, name="grp%s%d%d" % (nm, g, q), align_bytes=64)
                nc.vector.tensor_copy(out=t[:].rearrange("p (h c i) j -> p h c j i", h=2, i=4),
                                      in_=src[:].rearrange("p j (c i h) -> p h c j i", i=4, h=2))
                grouped[(nm, g, q)] = t

        def quantize_w(nm, q):
            for g in range(NG):
                nc.vector.quantize_mx(out=wcod[nm][:, g, CW * q:CW * (q + 1)].bitcast(FP8X4), scales=wscl[nm][:, g, CW * q:CW * (q + 1)],
                                      in_=grouped[(nm, g, q)][:].rearrange("p n j -> p (n j)"))

        xg = keep.tile([P, NG, 4 * TOK], BF16, name="xg", align_bytes=64)
        xgw = xg[:].rearrange("p g c -> p (g c)").bitcast(F32).rearrange("p (g r u) -> p g r u", g=NG, u=2)
        xcod = keep.tile([P, NG, TOK], U32, name="xcod", align_bytes=64)
        xscl = keep.tile([P, NG, TOK], U8, name="xscl", align_bytes=64)

        def turn_x():
            for a in range(NA):
                words = xs[:, a, :].bitcast(F32)
                xt = ptr.tile([P, NG, 2, P], F32, name="xt", tag="tr")
                for g in range(NG):
                    for u in range(2):
                        nc.tensor.transpose(xt[:, g, u, :], words[:, 256 * g + u:256 * (g + 1):2], ident[:])
                nc.scalar.copy(out=xgw[:, :, a * P:(a + 1) * P, :], in_=xt[:].rearrange("p g u r -> p g r u"))

        def quantize_x():
            for t0, tw in TOKEN_WINDOWS:
                for g in range(NG):
                    nc.vector.quantize_mx(out=xcod[:, g, t0:t0 + tw].bitcast(FP8X4), scales=xscl[:, g, t0:t0 + tw],
                                          in_=xg[:, g, 4 * t0:4 * (t0 + tw)])

        ut_ = {}
        dt_ = {}
        st_ = {}
        wt_ = {}
        lt_ = {}
        for q in range(NQ):
            ut_[q] = keep.tile([P, 2, 2, TOK], F32, name="uu%d" % q)
            dt_[q] = keep.tile([P, 2, 2, TOK], F32, name="dd%d" % q)
            st_[q] = keep.tile([P, 2, 2, TOK], F32, name="ss%d" % q)
            wt_[q] = keep.tile([P, 2, 2, TOK], F32, name="ww%d" % q)
            lt_[q] = keep.tile([P, 2, 2, TOK], F32, name="ll%d" % q)
        sums = {}

        def project_one(nm, q, bl, h, where):
            c0 = CW * q + 256 * h + P * bl
            cols = slice(c0, c0 + P)
            blk = 2 * q + bl
            dst, bias, mul = (ut_[q], biasv, -2.0) if nm == "v" else (dt_[q], biasm, 1.0)
            acc = where[0].tile([P, TOK], F32, name="acc" + nm, tag=where[1])
            for t0, tw in TOKEN_WINDOWS:
                for g in range(NG):
                    nc.tensor.matmul_mx(out=acc[:, t0:t0 + tw],
                                        lhsT=wcod[nm][:, g, cols].bitcast(FP8X4), lhsT_scale=wscl[nm][:, g, cols],
                                        rhs=xcod[:, g, t0:t0 + tw].bitcast(FP8X4), rhs_scale=xscl[:, g, t0:t0 + tw],
                                        start=(g == 0), stop=(g == NG - 1))
            nc.scalar.activation(out=dst[:, bl, h, :], in_=acc[:], func=AF.Relu, bias=bias[:, h, blk:blk + 1], scale=mul)

        def project(q, bl, h):
            project_one("v", q, bl, h, (pmx, "pv") if h == 0 else (psm, "s2"))
            project_one("m", q, bl, h, (pmx, "pm") if h == 0 else (psm, "s3"))

        def project_matrix(nm, q):
            banks = ((pmx, "pv"), (psm, "s2"), (pmx, "pm"), (psm, "s3"))
            for bl in range(2):
                for h in range(2):
                    project_one(nm, q, bl, h, banks[2 * bl + h])

        def flat(t, bl):
            return t[:, bl, :, :].rearrange("p g t -> p (g t)")

        def flat2(t):
            return t[:].rearrange("p g t -> p (g t)")

        def difference_u(q, bl):
            nc.vector.scalar_tensor_tensor(out=flat(ut_[q], bl), in0=flat(ut_[q], bl), scalar=4.0, in1=flat2(tblv),
                                           op0=ALU.min, op1=ALU.add)

        def difference_d(q, bl):
            nc.vector.scalar_tensor_tensor(out=flat(dt_[q], bl), in0=flat(dt_[q], bl), scalar=2.0, in1=flat2(m1p),
                                           op0=ALU.min, op1=ALU.subtract)

        def sigmoid(q, bl):
            nc.scalar.activation(out=flat(st_[q], bl), in_=flat(ut_[q], bl), func=AF.Sigmoid)

        def product_w(q, bl):
            nc.vector.tensor_tensor(out=flat(wt_[q], bl), in0=flat(dt_[q], bl), in1=flat(st_[q], bl), op=ALU.mult)

        def product_q1(q, bl):
            nc.vector.tensor_tensor(out=flat(dt_[q], bl), in0=flat(wt_[q], bl), in1=flat(dt_[q], bl), op=ALU.mult)

        def slab(t, a):
            return t[:, :, :, a * P:(a + 1) * P].rearrange("p b g t -> p (b g) t")

        def product_q1_tile(q, a):
            nc.vector.tensor_tensor(out=slab(dt_[q], a), in0=slab(wt_[q], a), in1=slab(dt_[q], a), op=ALU.mult)

        def product_q2_tile(q, a):
            nc.vector.tensor_tensor(out=dt_[q][:, :, :, a * P:(a + 1) * P], in0=dt_[q][:, :, :, a * P:(a + 1) * P],
                                    in1=nie1[:, :, a * P:(a + 1) * P].unsqueeze(1).to_broadcast([P, 2, 2, P]), op=ALU.mult)

        def product_q2(q, bl):
            nc.vector.tensor_tensor(out=flat(dt_[q], bl), in0=flat(dt_[q], bl), in1=flat2(nie1), op=ALU.mult)

        def turned_bank(k):
            if k % 4 < 2:
                return ptr.tile([P, 2, 256], F32, name="tb", tag="tr")
            return pmx.tile([P, 2, 256], F32, name="tb2", tag=("pm" if k % 4 == 2 else "pv"))

        def turn_unit(bank, src, a, table):
            spots = [(h, bl) for h in range(2) for bl in range(2)]
            tok = slice(a * P, (a + 1) * P)
            if table is not None:
                for k, (h, bl) in enumerate(spots):
                    nc.tensor.matmul(out=bank[:, h, bl * P:(bl + 1) * P], lhsT=table[:, h, tok], rhs=ident[:], is_transpose=True,
                                     start=(k == 0), stop=False)
            for k, (h, bl) in enumerate(spots):
                nc.tensor.matmul(out=bank[:, h, bl * P:(bl + 1) * P], lhsT=src[:, bl, h, tok], rhs=ident[:], is_transpose=True,
                                 start=(table is None and k == 0), stop=(k == len(spots) - 1))

        def mu_unit(q, a):
            bank = turned_bank(a) if q == NQ - 1 else ptr.tile([P, 2, 256], F32, name="tb", tag="tr")
            turn_unit(bank, wt_[q], a, m1p)
            res = stage.tile([P, CW], F32, name="mu", tag="mu")
            nc.scalar.activation(out=res[:].rearrange("p (r g) -> p r g", g=2), in_=bank[:].rearrange("p g r -> p r g"),
                                 func=AF.Copy, bias=-1.0, scale=1.0)
            nc.sync.dma_start(out=o1[:, a, CW * q:CW * (q + 1)], in_=res[:])

        def sum_region(q, a):
            if a < 2:
                return sums[(q, 0)][:, a, :]
            return sums[(q, 1)][:]

        def add_sums(q, src, tiles, first, last):
            if first:
                sums[(q, 0)] = psm.tile([P, 2, 256], F32, name="sumlo", tag="s%d" % (2 * q))
                sums[(q, 1)] = psm.tile([P, 256], F32, name="sumhi", tag="s%d" % (2 * q + 1))
            for a in tiles:
                region = sum_region(q, a)
                opens = first and a in (0, 2)
                closes = last and a in (1, 2)
                spots = [(bl, h) for bl in range(2) for h in range(2)]
                for k, (bl, h) in enumerate(spots):
                    nc.tensor.matmul(out=region[:, bl * P:(bl + 1) * P], lhsT=src[:, bl, h, a * P:(a + 1) * P], rhs=ident[:],
                                     is_transpose=True, start=(opens and k == 0), stop=(closes and k == len(spots) - 1))

        def log_unit(q, a):
            nc.scalar.activation(out=lt_[q][:, :, :, a * P:(a + 1) * P].rearrange("p b g t -> p (b g) t"),
                                 in_=st_[q][:, :, :, a * P:(a + 1) * P].rearrange("p b g t -> p (b g) t"),
                                 func=AF.Ln, scale=-1.0, bias=late_one[:, 0:1])

        def var_unit(q, a, k):
            bank = turned_bank(k) if q == NQ - 1 else ptr.tile([P, 2, 256], F32, name="tb", tag="tr")
            res = stage.tile([P, CW], F32, name="var", tag="var")
            if k in VAR_ON_SCALAR:
                turn_unit(bank, lt_[q], a, tblv)
                nc.scalar.activation(out=res[:].rearrange("p (r g) -> p r g", g=2), in_=bank[:].rearrange("p g r -> p r g"),
                                     func=AF.Copy, bias=1.0, scale=0.5)
                nc.sync.dma_start(out=o2[:, a, CW * q:CW * (q + 1)], in_=res[:])
                return
            turn_unit(bank, lt_[q], a, None)
            nc.vector.scalar_tensor_tensor(out=res[:].rearrange("p (i c g) -> p i c g", i=8, g=2),
                                           in0=bank[:].rearrange("p g (i c) -> p i c g", i=8), scalar=0.5,
                                           in1=v1x[:, a, :].rearrange("p (c g) -> p c g", g=2).unsqueeze(1).to_broadcast([P, 8, 32, 2]),
                                           op0=ALU.mult, op1=ALU.add)
            nc.sync.dma_start(out=o2[:, a, CW * q:CW * (q + 1)], in_=res[:])

        def scale_unit(q, a):
            res0 = stage.tile([P, 256], F32, name="sc", tag="sc")
            nc.vector.scalar_tensor_tensor(out=res0[:].rearrange("p (i c) -> p i c", i=8),
                                           in0=sum_region(q, a).rearrange("p (i c) -> p i c", i=8), scalar=0.5,
                                           in1=t0x[:, a, :].unsqueeze(1).to_broadcast([P, 8, 32]),
                                           op0=ALU.mult, op1=ALU.add)
            nc.sync.dma_start(out=o0[:, a, 256 * q:256 * (q + 1)], in_=res0[:])

        def chunk_main(q):
            for bl in range(2):
                for h in range(2):
                    project(q, bl, h)
            for bl in range(2):
                difference_u(q, bl)
                difference_d(q, bl)
                sigmoid(q, bl)
                product_w(q, bl)
            for a in range(NA):
                mu_unit(q, a)
            add_sums(q, ut_[q], range(NA), True, False)

        sv_flat = sv[:].rearrange("p a c -> p (a c)")
        nc.scalar.activation(out=sg[:], in_=sv_flat, func=AF.Sigmoid, scale=-2.0)
        nc.scalar.activation(out=sgc[:], in_=sv_flat, func=AF.Sigmoid, scale=2.0)
        compact_lay(0, 0, sv[:])
        compact_lay(0, 1, sm[:])
        compact_turn(0)
        table_back(0, 0, tblv)
        table_back(0, 1, m1p)
        nc.sync.dma_start(out=brow[0:4, :], in_=tcm_b.rearrange("(c q) -> c q", q=256))
        nc.sync.dma_start(out=brow[4:8, :], in_=tcv_b.rearrange("(c q) -> c q", q=256))
        nc.sync.dma_start(out=sw[:], in_=swv)
        load_m(1, 0)
        load_m(1, 1)
        nie_lay()
        compact_turn(1)
        table_back(1, 0, nie1)
        widen(0)
        interleave("m", 0)
        quantize_w("m", 0)
        turn_x()
        interleave("v", 0)
        quantize_x()
        quantize_w("v", 0)
        bias_columns()
        tables_small()
        widen(1)
        chunk_main(0)
        interleave("v", 1)
        quantize_w("v", 1)
        project_matrix("v", 1)
        for bl in range(2):
            difference_u(1, bl)
            sigmoid(1, bl)
        nc.scalar.activation(out=late_one[:], in_=st_[NQ - 1][:, 1, 1, 0:1], func=AF.Copy, scale=0.0, bias=1.0)
        interleave("m", 1)
        quantize_w("m", 1)
        project_matrix("m", 1)
        for bl in range(2):
            difference_d(1, bl)
            product_w(1, bl)
        for q in range(NQ):
            if q == 1:
                for a in range(NA):
                    mu_unit(1, a)
                add_sums(1, ut_[1], range(NA), True, False)
            for a in range(NA):
                log_unit(q, a)
                var_unit(q, a, NA * q + a)
            add_sums(q, lt_[q], range(NA), False, False)
            if q == 0:
                product_q1(q, 0)
                product_q1(q, 1)
                product_q2(q, 0)
                product_q2(q, 1)
                add_sums(q, dt_[q], range(NA), False, True)
                for a in range(NA):
                    scale_unit(q, a)
            else:
                for a in (2, 0, 1):
                    product_q1_tile(q, a)
                for a in (2, 0, 1):
                    product_q2_tile(q, a)
                    add_sums(q, dt_[q], (a,), False, True)
                    if a == 2:
                        scale_unit(q, 2)
                scale_unit(q, 0)
                scale_unit(q, 1)
